import numpy as np
import ml_dtypes


def mxq(x, axis, fmt="e4m3"):
    dtype, down = {"e4m3": (ml_dtypes.float8_e4m3fn, 7), "e5m2": (ml_dtypes.float8_e5m2, 14)}[fmt]
    v = np.moveaxis(np.asarray(x, np.float32).astype(ml_dtypes.bfloat16).astype(np.float64), axis, -1)
    blocks = v.reshape(v.shape[:-1] + (-1, 32))
    amax = np.abs(blocks).max(-1, keepdims=True)
    byte = np.maximum(np.where(amax > 0, np.frexp(amax)[1] - 1 + 127, 0) - down, 1)
    scale = np.exp2(byte - 127.0)
    codes = (blocks / scale).astype(np.float32).astype(dtype).astype(np.float64)
    return np.moveaxis((codes * scale).reshape(v.shape), -1, axis)


WIDE = False


def mx_kscale(k):
    if not WIDE:
        return np.ones(k)
    levels = np.array([10, -10, 5, -5, 0])
    a = np.random.permutation(np.resize(levels, k // 512 * 4)).reshape(k // 512, 4)
    idx = np.arange(k)
    return np.exp2(a[idx // 512, idx % 128 // 32])


BF16 = ml_dtypes.bfloat16


def bf(x):
    return np.asarray(x, np.float32).astype(BF16)


def f64(x):
    return np.asarray(x).astype(np.float64)


B, C, T, F, H, D = 8, 128, 512, 8, 2, 64
K = D * F
EPS = 1e-5


def conv_prelu_tln(x, W, b, a, lw, lb):
    y = (f64(W).reshape(H * D, C) @ f64(x).reshape(B, C, T * F)).reshape(B, H, D, T, F)
    y = y + f64(b)[None, :, :, None, None]
    y = np.where(y >= 0, y, f64(a)[None, :, None, None, None] * y)
    mu = y.mean(axis=(2, -1), keepdims=True)
    var = np.square(y - mu).mean(axis=(2, -1), keepdims=True)
    y = (y - mu) / np.sqrt(var + EPS)
    y = y * f64(lw)[None, :, :, None, :] + f64(lb)[None, :, :, None, :]
    return np.swapaxes(y, 2, 3).reshape(B, H, T, K)


def setup_inputs():
    n = np.random.standard_normal
    s = mx_kscale(K).reshape(D, F)
    return {"x": bf(n((B, C, T, F))),
            "Wq": bf(n((H, D, C)) / np.sqrt(C)), "bq": bf(0.2 * n((H, D))), "aq": bf(0.25 + 0.05 * n(H)),
            "lwq": bf((1.0 + 0.1 * n((H, D, F))) * s), "lbq": bf(0.2 * n((H, D, F)) * s),
            "Wk": bf(n((H, D, C)) / np.sqrt(C)), "bk": bf(0.2 * n((H, D))), "ak": bf(0.25 + 0.05 * n(H)),
            "lwk": bf((1.0 + 0.1 * n((H, D, F))) / s), "lbk": bf(0.2 * n((H, D, F)) / s)}


def reference(x, Wq, bq, aq, lwq, lbq, Wk, bk, ak, lwk, lbk):
    qf = conv_prelu_tln(x, Wq, bq, aq, lwq, lbq)
    kf = conv_prelu_tln(x, Wk, bk, ak, lwk, lbk)
    return (mxq(qf, 3, "e4m3") @ mxq(kf, 3, "e4m3").transpose(0, 1, 3, 2)) * (1.0 / np.sqrt(K))

@@ -1,0 +1,258 @@
+import math
+from contextlib import ExitStack
+
+import concourse.mybir as mybir
+from concourse.masks import make_identity
+
+F32 = mybir.dt.float32
+BF16 = mybir.dt.bfloat16
+U32 = mybir.dt.uint32
+U8 = mybir.dt.uint8
+FP8X4 = mybir.dt.float8_e4m3fn_x4
+ALU = mybir.AluOpType
+ACT = mybir.ActivationFunctionType
+
+B, C, T, F, H, D = 8, 128, 512, 8, 2, 64
+P = 128
+K = D * F
+PACK = 4
+EPS = 1e-5
+FRAME_TILES = T // P
+SIDES = 2 * H
+F_HI = F // PACK
+D_HI = D // PACK
+STATS = FRAME_TILES * SIDES
+
+FLOPS = 2 * (2 * H * D) * C * (B * T * F) + 2 * B * H * T * T * K
+
+
+def tile_multiheadselfattention_pa_t_kernel(
+    tc, x, Wq, bq, aq, lwq, lbq, Wk, bk, ak, lwk, lbk, out
+):
+    nc = tc.nc
+    with ExitStack() as ctx:
+        const = ctx.enter_context(tc.tile_pool(name="const", bufs=1))
+        x_pool = ctx.enter_context(tc.tile_pool(name="x", bufs=1))
+        act_pool = ctx.enter_context(tc.tile_pool(name="act", bufs=3))
+        junk_pool = ctx.enter_context(tc.tile_pool(name="junk", bufs=4))
+        stat_pool = ctx.enter_context(tc.tile_pool(name="stat", bufs=2))
+        plane_pool = ctx.enter_context(tc.tile_pool(name="plane", bufs=2))
+        code_pool = ctx.enter_context(tc.tile_pool(name="code", bufs=2))
+        store_pool = ctx.enter_context(tc.tile_pool(name="store", bufs=2))
+        conv_psum = ctx.enter_context(tc.psum_pool(name="conv_psum", bufs=2))
+        flip_psum = ctx.enter_context(tc.psum_pool(name="flip_psum", bufs=4))
+        score_psum = ctx.enter_context(tc.psum_pool(name="score_psum", bufs=2))
+
+        x_sb = []
+        for b in range(B):
+            x_b = x_pool.tile([P, T, F], BF16, name="x_b%d" % b)
+            nc.sync.dma_start(out=x_b[:], in_=x[b])
+            x_sb.append(x_b)
+
+        w_raw = const.tile([P, 2, C], BF16)
+        nc.scalar.dma_start(out=w_raw[:, 0, :], in_=Wq.rearrange("h d c -> (h d) c"))
+        nc.scalar.dma_start(out=w_raw[:, 1, :], in_=Wk.rearrange("h d c -> (h d) c"))
+        aq_raw = const.tile([P, H], BF16)
+        ak_raw = const.tile([P, H], BF16)
+        nc.scalar.dma_start(out=aq_raw[:], in_=aq.partition_broadcast(P))
+        nc.scalar.dma_start(out=ak_raw[:], in_=ak.partition_broadcast(P))
+        b_raw = const.tile([P, 2, H * D], BF16)
+        nc.scalar.dma_start(out=b_raw[:, 0, :], in_=bq.rearrange("h d -> (h d)").partition_broadcast(P))
+        nc.scalar.dma_start(out=b_raw[:, 1, :], in_=bk.rearrange("h d -> (h d)").partition_broadcast(P))
+        gs_raw = const.tile([P, K], BF16)
+        nc.vector.memset(gs_raw[:], 0.0)
+        nc.scalar.dma_start(out=gs_raw[0:2, :], in_=lwq.rearrange("h d f -> h (d f)"))
+        nc.scalar.dma_start(out=gs_raw[2:4, :], in_=lwk.rearrange("h d f -> h (d f)"))
+        nc.scalar.dma_start(out=gs_raw[4:6, :], in_=lbq.rearrange("h d f -> h (d f)"))
+        nc.scalar.dma_start(out=gs_raw[6:8, :], in_=lbk.rearrange("h d f -> h (d f)"))
+
+        ident = const.tile([P, P], F32)
+        make_identity(nc, ident[:])
+        eps_col = const.tile([P, 1], F32)
+        nc.vector.memset(eps_col[:], EPS)
+
+        slope = const.tile([P, SIDES], F32)
+        nc.vector.tensor_copy(out=slope[:, 0:H], in_=aq_raw[:])
+        nc.vector.tensor_copy(out=slope[:, H:SIDES], in_=ak_raw[:])
+        sign = const.tile([P, SIDES], F32)
+        nc.vector.tensor_scalar(out=sign[:], in0=slope[:], scalar1=1.0, scalar2=2.0, op0=ALU.is_le, op1=ALU.mult)
+        nc.vector.tensor_scalar_add(out=sign[:], in0=sign[:], scalar1=-1.0)
+
+        w_f32 = const.tile([P, 2, C], F32)
+        nc.vector.tensor_copy(out=w_f32[:], in_=w_raw[:])
+        w_flip = flip_psum.tile([P, T], F32, tag="flip")
+        for qk in range(2):
+            nc.tensor.transpose(out=w_flip[:, qk * P : (qk + 1) * P], in_=w_f32[:, qk, :], identity=ident[:])
+        w_t = const.tile([P, SIDES * D], BF16)
+        for side in range(SIDES):
+            cols = slice(side * D, (side + 1) * D)
+            nc.vector.tensor_scalar_mul(out=w_t[:, cols], in0=w_flip[:, cols], scalar1=sign[:, side : side + 1])
+
+        bias_t = const.tile([P, SIDES, D_HI, F_HI, PACK], F32)
+        for side in range(SIDES):
+            nc.vector.tensor_scalar_mul(
+                out=bias_t[:, side],
+                in0=b_raw[:, side // H, (side % H) * D : (side % H + 1) * D]
+                .rearrange("p (dh dl) -> p dh dl", dl=PACK)
+                .unsqueeze(2)
+                .to_broadcast([P, D_HI, F_HI, PACK]),
+                scalar1=sign[:, side : side + 1],
+            )
+
+        gs_rows = const.tile([P, PACK, D_HI, F_HI, PACK], F32)
+        gs_view = gs_raw[:].rearrange("p (dh dl fh j) -> p j dh fh dl", dl=PACK, fh=F_HI, j=PACK)
+        gs_flip = flip_psum.tile([P, T], F32, tag="flip")
+        for j in range(PACK):
+            nc.vector.tensor_copy(out=gs_rows[:, j], in_=gs_view[:, j])
+            nc.tensor.transpose(
+                out=gs_flip[:, j * P : (j + 1) * P],
+                in_=gs_rows[:, j].rearrange("p dh fh dl -> p (dh fh dl)"),
+                identity=ident[:],
+            )
+        gain_shift = const.tile([P, PACK, 2 * SIDES], F32)
+        nc.vector.tensor_copy(
+            out=gain_shift[:], in_=gs_flip[:].rearrange("p (j r) -> p j r", j=PACK)[:, :, 0 : 2 * SIDES]
+        )
+
+        acts = {}
+        sums = {}
+        mx_ops = {}
+
+        def convolve_and_activate(b):
+            act = act_pool.tile([P, FRAME_TILES, SIDES, PACK, P], F32, tag="act")
+            sum_p = stat_pool.tile([P, STATS], F32, tag="sum_p")
+            sum_pp = stat_pool.tile([P, STATS], F32, tag="sum_pp")
+            for ft in range(FRAME_TILES):
+                frames = slice(ft * P, (ft + 1) * P)
+                for j in range(PACK):
+                    bank = conv_psum.tile([P, SIDES * D_HI, F_HI, PACK], F32, tag="conv")
+                    for fh in range(F_HI):
+                        nc.tensor.matmul(
+                            out=bank[:, :, fh, :],
+                            lhsT=x_sb[b][:, frames, fh * PACK + j],
+                            rhs=w_t[:].rearrange("c (g dl) -> c g dl", dl=PACK),
+                            start=True,
+                            stop=True,
+                        )
+                    nc.vector.tensor_tensor(
+                        out=act[:, ft, :, j, :],
+                        in0=bank[:].rearrange("p (s dh) fh dl -> p s (dh fh dl)", s=SIDES),
+                        in1=bias_t[:].rearrange("p s dh fh dl -> p s (dh fh dl)"),
+                        op=ALU.add,
+                    )
+                for side in range(SIDES):
+                    col = ft * SIDES + side
+                    vals = act[:, ft, side].rearrange("p j r -> p (j r)")
+                    nc.vector.scalar_tensor_tensor(
+                        out=vals,
+                        in0=vals,
+                        scalar=slope[:, side : side + 1],
+                        in1=vals,
+                        op0=ALU.mult,
+                        op1=ALU.max,
+                        accum_out=sum_p[:, col : col + 1],
+                    )
+                    squares = junk_pool.tile([P, K], BF16, tag="squares")
+                    nc.scalar.activation(
+                        out=squares[:], in_=vals, func=ACT.Square, accum_out=sum_pp[:, col : col + 1]
+                    )
+            acts[b] = act
+            sums[b] = (sum_p, sum_pp)
+
+        def normalise(b):
+            sum_p, sum_pp = sums[b]
+            mean = stat_pool.tile([P, STATS], F32, tag="mean")
+            nc.vector.tensor_scalar_mul(out=mean[:], in0=sum_p[:], scalar1=1.0 / K)
+            mean_sq = stat_pool.tile([P, STATS], F32, tag="mean_sq")
+            nc.vector.tensor_tensor(out=mean_sq[:], in0=mean[:], in1=mean[:], op=ALU.mult)
+            var = stat_pool.tile([P, STATS], F32, tag="var")
+            nc.vector.scalar_tensor_tensor(
+                out=var[:], in0=sum_pp[:], scalar=1.0 / K, in1=mean_sq[:], op0=ALU.mult, op1=ALU.subtract
+            )
+            std = stat_pool.tile([P, STATS], F32, tag="std")
+            nc.scalar.activation(out=std[:], in_=var[:], func=ACT.Sqrt, bias=eps_col[:, 0:1])
+            rstd = stat_pool.tile([P, STATS], F32, tag="rstd")
+            nc.vector.reciprocal(out=rstd[:], in_=std[:])
+            factor = stat_pool.tile([P, STATS], F32, tag="factor")
+            nc.vector.tensor_tensor(
+                out=factor[:].rearrange("p (ft s) -> p ft s", s=SIDES),
+                in0=rstd[:].rearrange("p (ft s) -> p ft s", s=SIDES),
+                in1=sign[:].unsqueeze(1).to_broadcast([P, FRAME_TILES, SIDES]),
+                op=ALU.mult,
+            )
+            offset = stat_pool.tile([P, STATS], F32, tag="offset")
+            nc.vector.scalar_tensor_tensor(
+                out=offset[:], in0=mean[:], scalar=-1.0, in1=factor[:], op0=ALU.mult, op1=ALU.mult
+            )
+            for ft in range(FRAME_TILES):
+                for side in range(SIDES):
+                    col = ft * SIDES + side
+                    vals = acts[b][:, ft, side].rearrange("p j r -> p (j r)")
+                    nc.gpsimd.tensor_scalar(
+                        out=vals,
+                        in0=vals,
+                        scalar1=factor[:, col : col + 1],
+                        scalar2=offset[:, col : col + 1],
+                        op0=ALU.mult,
+                        op1=ALU.add,
+                    )
+
+        def quantise(b):
+            act = acts[b]
+            words = code_pool.tile([P, SIDES, T], U32, tag="words", align_bytes=64)
+            scales = code_pool.tile([P, SIDES, T], U8, tag="scales", align_bytes=64)
+            for side in range(SIDES):
+                planes = plane_pool.tile([P, PACK, T], BF16, tag="planes")
+                for j in range(PACK):
+                    flipped = flip_psum.tile([P, T], F32, tag="flip")
+                    for ft in range(FRAME_TILES):
+                        nc.tensor.transpose(
+                            out=flipped[:, ft * P : (ft + 1) * P], in_=act[:, ft, side, j, :], identity=ident[:]
+                        )
+                    nc.scalar.activation(
+                        out=planes[:, j, :],
+                        in_=flipped[:],
+                        func=ACT.Identity,
+                        scale=gain_shift[:, j, side : side + 1],
+                        bias=gain_shift[:, j, SIDES + side : SIDES + side + 1],
+                    )
+                grouped = plane_pool.tile([P, T, PACK], BF16, tag="grouped", align_bytes=64)
+                nc.vector.tensor_copy(
+                    out=grouped[:].rearrange("p (c i) j -> p c j i", i=4),
+                    in_=planes[:].rearrange("p j (c i) -> p c j i", i=4),
+                )
+                nc.vector.quantize_mx(
+                    out=words[:, side, :].bitcast(FP8X4),
+                    scales=scales[:, side, :],
+                    in_=grouped[:].rearrange("p t j -> p (t j)"),
+                )
+            mx_ops[b] = (words, scales)
+
+        def score(b):
+            words, scales = mx_ops[b]
+            for h in range(H):
+                result = store_pool.tile([P, FRAME_TILES, T], F32, tag="result")
+                for ft in range(FRAME_TILES):
+                    frames = slice(ft * P, (ft + 1) * P)
+                    bank = score_psum.tile([P, T], F32, tag="score")
+                    nc.tensor.matmul_mx(
+                        out=bank[:],
+                        lhsT=words[:, h, frames].bitcast(FP8X4),
+                        lhsT_scale=scales[:, h, frames],
+                        rhs=words[:, H + h, :].bitcast(FP8X4),
+                        rhs_scale=scales[:, H + h, :],
+                        start=True,
+                        stop=True,
+                    )
+                    nc.scalar.activation(out=result[:, ft, :], in_=bank[:], func=ACT.Copy, scale=1.0 / math.sqrt(K))
+                nc.sync.dma_start(out=out[b, h].rearrange("(ft p) s -> p ft s", p=P), in_=result[:])
+
+        for step in range(B + 3):
+            if 0 <= step - 1 < B:
+                normalise(step - 1)
+            if 0 <= step - 2 < B:
+                quantise(step - 2)
+            if 0 <= step - 3 < B:
+                score(step - 3)
+            if step < B:
+                convolve_and_activate(step)

@@ -43,12 +43,6 @@ def tile_multiheadselfattention_pa_t_kernel(
         flip_psum = ctx.enter_context(tc.psum_pool(name="flip_psum", bufs=4))
         score_psum = ctx.enter_context(tc.psum_pool(name="score_psum", bufs=2))
 
-        x_sb = []
-        for b in range(B):
-            x_b = x_pool.tile([P, T, F], BF16, name="x_b%d" % b)
-            nc.sync.dma_start(out=x_b[:], in_=x[b])
-            x_sb.append(x_b)
-
         w_raw = const.tile([P, 2, C], BF16)
         nc.scalar.dma_start(out=w_raw[:, 0, :], in_=Wq.rearrange("h d c -> (h d) c"))
         nc.scalar.dma_start(out=w_raw[:, 1, :], in_=Wk.rearrange("h d c -> (h d) c"))
@@ -66,14 +60,23 @@ def tile_multiheadselfattention_pa_t_kernel(
         nc.scalar.dma_start(out=gs_raw[4:6, :], in_=lbq.rearrange("h d f -> h (d f)"))
         nc.scalar.dma_start(out=gs_raw[6:8, :], in_=lbk.rearrange("h d f -> h (d f)"))
 
+        x_sb = []
+        for b in range(B):
+            x_b = x_pool.tile([P, T, F], BF16, name="x_b%d" % b)
+            for ft in range(FRAME_TILES):
+                frames = slice(ft * P, (ft + 1) * P)
+                nc.sync.dma_start(out=x_b[:, frames, :], in_=x[b, :, frames, :])
+            x_sb.append(x_b)
+
         ident = const.tile([P, P], F32)
         make_identity(nc, ident[:])
         eps_col = const.tile([P, 1], F32)
         nc.vector.memset(eps_col[:], EPS)
 
         slope = const.tile([P, SIDES], F32)
-        nc.vector.tensor_copy(out=slope[:, 0:H], in_=aq_raw[:])
-        nc.vector.tensor_copy(out=slope[:, H:SIDES], in_=ak_raw[:])
+        slope_by_head = slope[:].rearrange("p (h qk) -> p h qk", qk=2)
+        nc.vector.tensor_copy(out=slope_by_head[:, :, 0], in_=aq_raw[:])
+        nc.vector.tensor_copy(out=slope_by_head[:, :, 1], in_=ak_raw[:])
         sign = const.tile([P, SIDES], F32)
         nc.vector.tensor_scalar(out=sign[:], in0=slope[:], scalar1=1.0, scalar2=2.0, op0=ALU.is_le, op1=ALU.mult)
         nc.vector.tensor_scalar_add(out=sign[:], in0=sign[:], scalar1=-1.0)
@@ -85,14 +88,19 @@ def tile_multiheadselfattention_pa_t_kernel(
             nc.tensor.transpose(out=w_flip[:, qk * P : (qk + 1) * P], in_=w_f32[:, qk, :], identity=ident[:])
         w_t = const.tile([P, SIDES * D], BF16)
         for side in range(SIDES):
-            cols = slice(side * D, (side + 1) * D)
-            nc.vector.tensor_scalar_mul(out=w_t[:, cols], in0=w_flip[:, cols], scalar1=sign[:, side : side + 1])
+            h, qk = divmod(side, 2)
+            nc.vector.tensor_scalar_mul(
+                out=w_t[:, side * D : (side + 1) * D],
+                in0=w_flip[:, (qk * H + h) * D : (qk * H + h + 1) * D],
+                scalar1=sign[:, side : side + 1],
+            )
 
         bias_t = const.tile([P, SIDES, D_HI, F_HI, PACK], F32)
         for side in range(SIDES):
+            h, qk = divmod(side, 2)
             nc.vector.tensor_scalar_mul(
                 out=bias_t[:, side],
-                in0=b_raw[:, side // H, (side % H) * D : (side % H + 1) * D]
+                in0=b_raw[:, qk, h * D : (h + 1) * D]
                 .rearrange("p (dh dl) -> p dh dl", dl=PACK)
                 .unsqueeze(2)
                 .to_broadcast([P, D_HI, F_HI, PACK]),
@@ -116,50 +124,56 @@ def tile_multiheadselfattention_pa_t_kernel(
 
         acts = {}
         sums = {}
+        norms = {}
+        flips = {}
+        planes_of = {}
         mx_ops = {}
+        results = {}
 
-        def convolve_and_activate(b):
-            act = act_pool.tile([P, FRAME_TILES, SIDES, PACK, P], F32, tag="act")
-            sum_p = stat_pool.tile([P, STATS], F32, tag="sum_p")
-            sum_pp = stat_pool.tile([P, STATS], F32, tag="sum_pp")
-            for ft in range(FRAME_TILES):
-                frames = slice(ft * P, (ft + 1) * P)
-                for j in range(PACK):
-                    bank = conv_psum.tile([P, SIDES * D_HI, F_HI, PACK], F32, tag="conv")
-                    for fh in range(F_HI):
-                        nc.tensor.matmul(
-                            out=bank[:, :, fh, :],
-                            lhsT=x_sb[b][:, frames, fh * PACK + j],
-                            rhs=w_t[:].rearrange("c (g dl) -> c g dl", dl=PACK),
-                            start=True,
-                            stop=True,
-                        )
-                    nc.vector.tensor_tensor(
-                        out=act[:, ft, :, j, :],
-                        in0=bank[:].rearrange("p (s dh) fh dl -> p s (dh fh dl)", s=SIDES),
-                        in1=bias_t[:].rearrange("p s dh fh dl -> p s (dh fh dl)"),
-                        op=ALU.add,
+        def convolve(b, ft):
+            if ft == 0:
+                acts[b] = act_pool.tile([P, FRAME_TILES, SIDES, PACK, P], F32, name="act", tag="act")
+                sums[b] = (
+                    stat_pool.tile([P, STATS], F32, name="sum_p", tag="sum_p"),
+                    stat_pool.tile([P, STATS], F32, name="sum_pp", tag="sum_pp"),
+                )
+            act = acts[b]
+            sum_p, sum_pp = sums[b]
+            frames = slice(ft * P, (ft + 1) * P)
+            for j in range(PACK):
+                bank = conv_psum.tile([P, SIDES * D_HI, F_HI, PACK], F32, tag="conv")
+                for fh in range(F_HI):
+                    nc.tensor.matmul(
+                        out=bank[:, :, fh, :],
+                        lhsT=x_sb[b][:, frames, fh * PACK + j],
+                        rhs=w_t[:].rearrange("c (g dl) -> c g dl", dl=PACK),
+                        start=True,
+                        stop=True,
                     )
-                for side in range(SIDES):
-                    col = ft * SIDES + side
-                    vals = act[:, ft, side].rearrange("p j r -> p (j r)")
-                    nc.vector.scalar_tensor_tensor(
-                        out=vals,
-                        in0=vals,
-                        scalar=slope[:, side : side + 1],
-                        in1=vals,
-                        op0=ALU.mult,
-                        op1=ALU.max,
-                        accum_out=sum_p[:, col : col + 1],
-                    )
-                    squares = junk_pool.tile([P, K], BF16, tag="squares")
-                    nc.scalar.activation(
-                        out=squares[:], in_=vals, func=ACT.Square, accum_out=sum_pp[:, col : col + 1]
-                    )
-            acts[b] = act
-            sums[b] = (sum_p, sum_pp)
+                nc.vector.tensor_tensor(
+                    out=act[:, ft, :, j, :],
+                    in0=bank[:].rearrange("p (s dh) fh dl -> p s (dh fh dl)", s=SIDES),
+                    in1=bias_t[:].rearrange("p s dh fh dl -> p s (dh fh dl)"),
+                    op=ALU.add,
+                )
+            for side in range(SIDES):
+                col = ft * SIDES + side
+                vals = act[:, ft, side].rearrange("p j r -> p (j r)")
+                nc.vector.scalar_tensor_tensor(
+                    out=vals,
+                    in0=vals,
+                    scalar=slope[:, side : side + 1],
+                    in1=vals,
+                    op0=ALU.mult,
+                    op1=ALU.max,
+                    accum_out=sum_p[:, col : col + 1],
+                )
+                squares = junk_pool.tile([P, K], BF16, tag="squares")
+                nc.scalar.activation(
+                    out=squares[:], in_=vals, func=ACT.Square, accum_out=sum_pp[:, col : col + 1]
+                )
 
-        def normalise(b):
+        def statistics(b):
             sum_p, sum_pp = sums[b]
             mean = stat_pool.tile([P, STATS], F32, tag="mean")
             nc.vector.tensor_scalar_mul(out=mean[:], in0=sum_p[:], scalar1=1.0 / K)
@@ -184,75 +198,102 @@ def tile_multiheadselfattention_pa_t_kernel(
             nc.vector.scalar_tensor_tensor(
                 out=offset[:], in0=mean[:], scalar=-1.0, in1=factor[:], op0=ALU.mult, op1=ALU.mult
             )
+            norms[b] = (factor, offset)
+
+        def normalise(b, side):
+            factor, offset = norms[b]
             for ft in range(FRAME_TILES):
-                for side in range(SIDES):
-                    col = ft * SIDES + side
-                    vals = acts[b][:, ft, side].rearrange("p j r -> p (j r)")
-                    nc.gpsimd.tensor_scalar(
-                        out=vals,
-                        in0=vals,
-                        scalar1=factor[:, col : col + 1],
-                        scalar2=offset[:, col : col + 1],
-                        op0=ALU.mult,
-                        op1=ALU.add,
-                    )
-
-        def quantise(b):
-            act = acts[b]
-            words = code_pool.tile([P, SIDES, T], U32, tag="words", align_bytes=64)
-            scales = code_pool.tile([P, SIDES, T], U8, tag="scales", align_bytes=64)
-            for side in range(SIDES):
-                planes = plane_pool.tile([P, PACK, T], BF16, tag="planes")
-                for j in range(PACK):
-                    flipped = flip_psum.tile([P, T], F32, tag="flip")
-                    for ft in range(FRAME_TILES):
-                        nc.tensor.transpose(
-                            out=flipped[:, ft * P : (ft + 1) * P], in_=act[:, ft, side, j, :], identity=ident[:]
-                        )
-                    nc.scalar.activation(
-                        out=planes[:, j, :],
-                        in_=flipped[:],
-                        func=ACT.Identity,
-                        scale=gain_shift[:, j, side : side + 1],
-                        bias=gain_shift[:, j, SIDES + side : SIDES + side + 1],
-                    )
-                grouped = plane_pool.tile([P, T, PACK], BF16, tag="grouped", align_bytes=64)
-                nc.vector.tensor_copy(
-                    out=grouped[:].rearrange("p (c i) j -> p c j i", i=4),
-                    in_=planes[:].rearrange("p j (c i) -> p c j i", i=4),
+                col = ft * SIDES + side
+                vals = acts[b][:, ft, side].rearrange("p j r -> p (j r)")
+                nc.gpsimd.tensor_scalar(
+                    out=vals,
+                    in0=vals,
+                    scalar1=factor[:, col : col + 1],
+                    scalar2=offset[:, col : col + 1],
+                    op0=ALU.mult,
+                    op1=ALU.add,
                 )
-                nc.vector.quantize_mx(
-                    out=words[:, side, :].bitcast(FP8X4),
-                    scales=scales[:, side, :],
-                    in_=grouped[:].rearrange("p t j -> p (t j)"),
-                )
-            mx_ops[b] = (words, scales)
 
-        def score(b):
-            words, scales = mx_ops[b]
-            for h in range(H):
-                result = store_pool.tile([P, FRAME_TILES, T], F32, tag="result")
+        def flip(b, side):
+            banks = []
+            for j in range(PACK):
+                flipped = flip_psum.tile([P, T], F32, name="flipped", tag="flip")
                 for ft in range(FRAME_TILES):
-                    frames = slice(ft * P, (ft + 1) * P)
-                    bank = score_psum.tile([P, T], F32, tag="score")
-                    nc.tensor.matmul_mx(
-                        out=bank[:],
-                        lhsT=words[:, h, frames].bitcast(FP8X4),
-                        lhsT_scale=scales[:, h, frames],
-                        rhs=words[:, H + h, :].bitcast(FP8X4),
-                        rhs_scale=scales[:, H + h, :],
-                        start=True,
-                        stop=True,
+                    nc.tensor.transpose(
+                        out=flipped[:, ft * P : (ft + 1) * P], in_=acts[b][:, ft, side, j, :], identity=ident[:]
                     )
-                    nc.scalar.activation(out=result[:, ft, :], in_=bank[:], func=ACT.Copy, scale=1.0 / math.sqrt(K))
+                banks.append(flipped)
+            flips[(b, side)] = banks
+
+        def gain_and_shift(b, side):
+            h, qk = divmod(side, 2)
+            planes = plane_pool.tile([P, PACK, T], BF16, tag="planes")
+            for j in range(PACK):
+                nc.scalar.activation(
+                    out=planes[:, j, :],
+                    in_=flips[(b, side)][j][:],
+                    func=ACT.Identity,
+                    scale=gain_shift[:, j, qk * H + h : qk * H + h + 1],
+                    bias=gain_shift[:, j, SIDES + qk * H + h : SIDES + qk * H + h + 1],
+                )
+            planes_of[(b, side)] = planes
+
+        def quantise(b, side):
+            if side == 0:
+                mx_ops[b] = (
+                    code_pool.tile([P, SIDES, T], U32, name="words", tag="words", align_bytes=64),
+                    code_pool.tile([P, SIDES, T], U8, name="scales", tag="scales", align_bytes=64),
+                )
+            words, scales = mx_ops[b]
+            grouped = plane_pool.tile([P, T, PACK], BF16, tag="grouped", align_bytes=64)
+            nc.vector.tensor_copy(
+                out=grouped[:].rearrange("p (c i) j -> p c j i", i=4),
+                in_=planes_of[(b, side)][:].rearrange("p j (c i) -> p c j i", i=4),
+            )
+            nc.vector.quantize_mx(
+                out=words[:, side, :].bitcast(FP8X4),
+                scales=scales[:, side, :],
+                in_=grouped[:].rearrange("p t j -> p (t j)"),
+            )
+
+        def score(b, h, half):
+            words, scales = mx_ops[b]
+            if half == 0:
+                results[(b, h)] = store_pool.tile([P, FRAME_TILES, T], F32, name="result", tag="result")
+            result = results[(b, h)]
+            for ft in (2 * half, 2 * half + 1):
+                frames = slice(ft * P, (ft + 1) * P)
+                bank = score_psum.tile([P, T], F32, tag="score")
+                nc.tensor.matmul_mx(
+                    out=bank[:],
+                    lhsT=words[:, 2 * h, frames].bitcast(FP8X4),
+                    lhsT_scale=scales[:, 2 * h, frames],
+                    rhs=words[:, 2 * h + 1, :].bitcast(FP8X4),
+                    rhs_scale=scales[:, 2 * h + 1, :],
+                    start=True,
+                    stop=True,
+                )
+                nc.scalar.activation(out=result[:, ft, :], in_=bank[:], func=ACT.Copy, scale=1.0 / math.sqrt(K))
+            if half == 1:
                 nc.sync.dma_start(out=out[b, h].rearrange("(ft p) s -> p ft s", p=P), in_=result[:])
 
-        for step in range(B + 3):
-            if 0 <= step - 1 < B:
-                normalise(step - 1)
-            if 0 <= step - 2 < B:
-                quantise(step - 2)
-            if 0 <= step - 3 < B:
-                score(step - 3)
-            if step < B:
-                convolve_and_activate(step)
+        def unit(n):
+            return n // 4 - 1, n % 4
+
+        with tc.manual_schedule():
+            for n in range(4 * (B + 2)):
+                b, i = divmod(n, 4)
+                if i == 0 and 0 <= b - 1 < B:
+                    statistics(b - 1)
+                if 0 <= b - 1 < B:
+                    normalise(b - 1, i)
+                if 0 <= unit(n - 2)[0] < B:
+                    gain_and_shift(*unit(n - 2))
+                if 0 <= b - 2 < B:
+                    score(b - 2, i // 2, i % 2)
+                if b < B:
+                    convolve(b, i)
+                if 0 <= unit(n - 1)[0] < B:
+                    flip(*unit(n - 1))
+                if 0 <= unit(n - 2)[0] < B:
+                    quantise(*unit(n - 2))

@@ -39,8 +39,8 @@ def tile_multiheadselfattention_pa_t_kernel(
         plane_pool = ctx.enter_context(tc.tile_pool(name="plane", bufs=2))
         code_pool = ctx.enter_context(tc.tile_pool(name="code", bufs=2))
         store_pool = ctx.enter_context(tc.tile_pool(name="store", bufs=2))
-        conv_psum = ctx.enter_context(tc.psum_pool(name="conv_psum", bufs=2))
-        flip_psum = ctx.enter_context(tc.psum_pool(name="flip_psum", bufs=4))
+        conv_psum = ctx.enter_context(tc.psum_pool(name="conv_psum", bufs=3))
+        flip_psum = ctx.enter_context(tc.psum_pool(name="flip_psum", bufs=3))
         score_psum = ctx.enter_context(tc.psum_pool(name="score_psum", bufs=2))
 
         w_raw = const.tile([P, 2, C], BF16)
@@ -127,53 +127,52 @@ def tile_multiheadselfattention_pa_t_kernel(
         norms = {}
         flips = {}
         planes_of = {}
+        grouped_of = {}
         mx_ops = {}
+        score_banks = {}
         results = {}
 
-        def convolve(b, ft):
-            if ft == 0:
+        def convolve(b, ft, j):
+            if ft == 0 and j == 0:
                 acts[b] = act_pool.tile([P, FRAME_TILES, SIDES, PACK, P], F32, name="act", tag="act")
+            bank = conv_psum.tile([P, SIDES * D_HI, F_HI, PACK], F32, tag="conv")
+            for fh in range(F_HI):
+                nc.tensor.matmul(
+                    out=bank[:, :, fh, :],
+                    lhsT=x_sb[b][:, ft * P : (ft + 1) * P, fh * PACK + j],
+                    rhs=w_t[:].rearrange("c (g dl) -> c g dl", dl=PACK),
+                    start=True,
+                    stop=True,
+                )
+            nc.vector.tensor_tensor(
+                out=acts[b][:, ft, :, j, :],
+                in0=bank[:].rearrange("p (s dh) fh dl -> p s (dh fh dl)", s=SIDES),
+                in1=bias_t[:].rearrange("p s dh fh dl -> p s (dh fh dl)"),
+                op=ALU.add,
+            )
+
+        def activate(b, ft, side):
+            if ft == 0 and side == 0:
                 sums[b] = (
                     stat_pool.tile([P, STATS], F32, name="sum_p", tag="sum_p"),
                     stat_pool.tile([P, STATS], F32, name="sum_pp", tag="sum_pp"),
                 )
-            act = acts[b]
             sum_p, sum_pp = sums[b]
-            frames = slice(ft * P, (ft + 1) * P)
-            for j in range(PACK):
-                bank = conv_psum.tile([P, SIDES * D_HI, F_HI, PACK], F32, tag="conv")
-                for fh in range(F_HI):
-                    nc.tensor.matmul(
-                        out=bank[:, :, fh, :],
-                        lhsT=x_sb[b][:, frames, fh * PACK + j],
-                        rhs=w_t[:].rearrange("c (g dl) -> c g dl", dl=PACK),
-                        start=True,
-                        stop=True,
-                    )
-                nc.vector.tensor_tensor(
-                    out=act[:, ft, :, j, :],
-                    in0=bank[:].rearrange("p (s dh) fh dl -> p s (dh fh dl)", s=SIDES),
-                    in1=bias_t[:].rearrange("p s dh fh dl -> p s (dh fh dl)"),
-                    op=ALU.add,
-                )
-            for side in range(SIDES):
-                col = ft * SIDES + side
-                vals = act[:, ft, side].rearrange("p j r -> p (j r)")
-                nc.vector.scalar_tensor_tensor(
-                    out=vals,
-                    in0=vals,
-                    scalar=slope[:, side : side + 1],
-                    in1=vals,
-                    op0=ALU.mult,
-                    op1=ALU.max,
-                    accum_out=sum_p[:, col : col + 1],
-                )
-                squares = junk_pool.tile([P, K], BF16, tag="squares")
-                nc.scalar.activation(
-                    out=squares[:], in_=vals, func=ACT.Square, accum_out=sum_pp[:, col : col + 1]
-                )
+            col = ft * SIDES + side
+            vals = acts[b][:, ft, side].rearrange("p j r -> p (j r)")
+            nc.vector.scalar_tensor_tensor(
+                out=vals,
+                in0=vals,
+                scalar=slope[:, side : side + 1],
+                in1=vals,
+                op0=ALU.mult,
+                op1=ALU.max,
+                accum_out=sum_p[:, col : col + 1],
+            )
+            squares = junk_pool.tile([P, K], BF16, tag="squares")
+            nc.scalar.activation(out=squares[:], in_=vals, func=ACT.Square, accum_out=sum_pp[:, col : col + 1])
 
-        def statistics(b):
+        def deviation(b):
             sum_p, sum_pp = sums[b]
             mean = stat_pool.tile([P, STATS], F32, tag="mean")
             nc.vector.tensor_scalar_mul(out=mean[:], in0=sum_p[:], scalar1=1.0 / K)
@@ -185,6 +184,10 @@ def tile_multiheadselfattention_pa_t_kernel(
             )
             std = stat_pool.tile([P, STATS], F32, tag="std")
             nc.scalar.activation(out=std[:], in_=var[:], func=ACT.Sqrt, bias=eps_col[:, 0:1])
+            norms[b] = (mean, std)
+
+        def factors(b):
+            mean, std = norms[b]
             rstd = stat_pool.tile([P, STATS], F32, tag="rstd")
             nc.vector.reciprocal(out=rstd[:], in_=std[:])
             factor = stat_pool.tile([P, STATS], F32, tag="factor")
@@ -200,12 +203,12 @@ def tile_multiheadselfattention_pa_t_kernel(
             )
             norms[b] = (factor, offset)
 
-        def normalise(b, side):
+        def normalise(b, side, ft):
             factor, offset = norms[b]
-            for ft in range(FRAME_TILES):
-                col = ft * SIDES + side
-                vals = acts[b][:, ft, side].rearrange("p j r -> p (j r)")
-                nc.gpsimd.tensor_scalar(
+            col = ft * SIDES + side
+            vals = acts[b][:, ft, side].rearrange("p j r -> p (j r)")
+            if ft % 2 == 0:
+                nc.vector.tensor_scalar(
                     out=vals,
                     in0=vals,
                     scalar1=factor[:, col : col + 1],
@@ -213,30 +216,42 @@ def tile_multiheadselfattention_pa_t_kernel(
                     op0=ALU.mult,
                     op1=ALU.add,
                 )
-
-        def flip(b, side):
-            banks = []
-            for j in range(PACK):
-                flipped = flip_psum.tile([P, T], F32, name="flipped", tag="flip")
-                for ft in range(FRAME_TILES):
-                    nc.tensor.transpose(
-                        out=flipped[:, ft * P : (ft + 1) * P], in_=acts[b][:, ft, side, j, :], identity=ident[:]
-                    )
-                banks.append(flipped)
-            flips[(b, side)] = banks
-
-        def gain_and_shift(b, side):
-            h, qk = divmod(side, 2)
-            planes = plane_pool.tile([P, PACK, T], BF16, tag="planes")
-            for j in range(PACK):
+            else:
                 nc.scalar.activation(
-                    out=planes[:, j, :],
-                    in_=flips[(b, side)][j][:],
+                    out=vals,
+                    in_=vals,
                     func=ACT.Identity,
-                    scale=gain_shift[:, j, qk * H + h : qk * H + h + 1],
-                    bias=gain_shift[:, j, SIDES + qk * H + h : SIDES + qk * H + h + 1],
+                    scale=factor[:, col : col + 1],
+                    bias=offset[:, col : col + 1],
                 )
-            planes_of[(b, side)] = planes
+
+        def flip(b, side, j):
+            flipped = flip_psum.tile([P, T], F32, tag="flip")
+            for ft in range(FRAME_TILES):
+                nc.tensor.transpose(
+                    out=flipped[:, ft * P : (ft + 1) * P], in_=acts[b][:, ft, side, j, :], identity=ident[:]
+                )
+            flips[(b, side, j)] = flipped
+
+        def gain_and_shift(b, side, j):
+            if j == 0:
+                planes_of[(b, side)] = plane_pool.tile([P, PACK, T], BF16, name="planes", tag="planes")
+            h, qk = divmod(side, 2)
+            nc.scalar.activation(
+                out=planes_of[(b, side)][:, j, :],
+                in_=flips[(b, side, j)][:],
+                func=ACT.Identity,
+                scale=gain_shift[:, j, qk * H + h : qk * H + h + 1],
+                bias=gain_shift[:, j, SIDES + qk * H + h : SIDES + qk * H + h + 1],
+            )
+
+        def regroup(b, side):
+            grouped = plane_pool.tile([P, T, PACK], BF16, tag="grouped", align_bytes=64)
+            nc.vector.tensor_copy(
+                out=grouped[:].rearrange("p (c i) j -> p c j i", i=4),
+                in_=planes_of[(b, side)][:].rearrange("p j (c i) -> p c j i", i=4),
+            )
+            grouped_of[(b, side)] = grouped
 
         def quantise(b, side):
             if side == 0:
@@ -245,55 +260,83 @@ def tile_multiheadselfattention_pa_t_kernel(
                     code_pool.tile([P, SIDES, T], U8, name="scales", tag="scales", align_bytes=64),
                 )
             words, scales = mx_ops[b]
-            grouped = plane_pool.tile([P, T, PACK], BF16, tag="grouped", align_bytes=64)
-            nc.vector.tensor_copy(
-                out=grouped[:].rearrange("p (c i) j -> p c j i", i=4),
-                in_=planes_of[(b, side)][:].rearrange("p j (c i) -> p c j i", i=4),
-            )
             nc.vector.quantize_mx(
                 out=words[:, side, :].bitcast(FP8X4),
                 scales=scales[:, side, :],
-                in_=grouped[:].rearrange("p t j -> p (t j)"),
+                in_=grouped_of[(b, side)][:].rearrange("p t j -> p (t j)"),
             )
 
-        def score(b, h, half):
+        def score(b, h, ft):
             words, scales = mx_ops[b]
-            if half == 0:
+            frames = slice(ft * P, (ft + 1) * P)
+            bank = score_psum.tile([P, T], F32, tag="score")
+            nc.tensor.matmul_mx(
+                out=bank[:],
+                lhsT=words[:, 2 * h, frames].bitcast(FP8X4),
+                lhsT_scale=scales[:, 2 * h, frames],
+                rhs=words[:, 2 * h + 1, :].bitcast(FP8X4),
+                rhs_scale=scales[:, 2 * h + 1, :],
+                start=True,
+                stop=True,
+            )
+            score_banks[(b, h, ft)] = bank
+
+        def scale_and_store(b, h, ft):
+            if ft == 0:
                 results[(b, h)] = store_pool.tile([P, FRAME_TILES, T], F32, name="result", tag="result")
             result = results[(b, h)]
-            for ft in (2 * half, 2 * half + 1):
-                frames = slice(ft * P, (ft + 1) * P)
-                bank = score_psum.tile([P, T], F32, tag="score")
-                nc.tensor.matmul_mx(
-                    out=bank[:],
-                    lhsT=words[:, 2 * h, frames].bitcast(FP8X4),
-                    lhsT_scale=scales[:, 2 * h, frames],
-                    rhs=words[:, 2 * h + 1, :].bitcast(FP8X4),
-                    rhs_scale=scales[:, 2 * h + 1, :],
-                    start=True,
-                    stop=True,
-                )
-                nc.scalar.activation(out=result[:, ft, :], in_=bank[:], func=ACT.Copy, scale=1.0 / math.sqrt(K))
-            if half == 1:
+            nc.scalar.activation(
+                out=result[:, ft, :], in_=score_banks[(b, h, ft)][:], func=ACT.Copy, scale=1.0 / math.sqrt(K)
+            )
+            if ft == FRAME_TILES - 1:
                 nc.sync.dma_start(out=out[b, h].rearrange("(ft p) s -> p ft s", p=P), in_=result[:])
 
-        def unit(n):
-            return n // 4 - 1, n % 4
+        TICKS = FRAME_TILES * PACK
+        LAG_ACTIVATE = 4
+        LAG_DEVIATION = LAG_ACTIVATE + TICKS + 1
+        LAG_FACTORS = LAG_DEVIATION + 1
+        LAG_NORMALISE = LAG_FACTORS + 1
+        LAG_FLIP = LAG_NORMALISE + 5
+        LAG_GAIN = LAG_FLIP + 1
+        LAG_REGROUP = LAG_GAIN + 4
+        LAG_QUANTISE = LAG_REGROUP + 2
+        LAG_SCORE = LAG_QUANTISE + 6
+        LAG_STORE = LAG_SCORE + 1
+
+        def piece(tick, lag):
+            b, rest = divmod(tick - lag, TICKS)
+            return (b,) + divmod(rest, 4)
 
         with tc.manual_schedule():
-            for n in range(4 * (B + 2)):
-                b, i = divmod(n, 4)
-                if i == 0 and 0 <= b - 1 < B:
-                    statistics(b - 1)
-                if 0 <= b - 1 < B:
-                    normalise(b - 1, i)
-                if 0 <= unit(n - 2)[0] < B:
-                    gain_and_shift(*unit(n - 2))
-                if 0 <= b - 2 < B:
-                    score(b - 2, i // 2, i % 2)
-                if b < B:
-                    convolve(b, i)
-                if 0 <= unit(n - 1)[0] < B:
-                    flip(*unit(n - 1))
-                if 0 <= unit(n - 2)[0] < B:
-                    quantise(*unit(n - 2))
+            for tick in range(B * TICKS + LAG_STORE):
+                b, ft, j = piece(tick, 0)
+                if 0 <= b < B:
+                    convolve(b, ft, j)
+                b, side, j = piece(tick, LAG_FLIP)
+                if 0 <= b < B:
+                    flip(b, side, j)
+                b, pair, odd = piece(tick, LAG_SCORE)
+                if 0 <= b < B and odd % 2 == 0:
+                    score(b, pair // 2, 2 * (pair % 2) + odd // 2)
+                b, side, j = piece(tick, LAG_GAIN)
+                if 0 <= b < B:
+                    gain_and_shift(b, side, j)
+                b, pair, odd = piece(tick, LAG_STORE)
+                if 0 <= b < B and odd % 2 == 0:
+                    scale_and_store(b, pair // 2, 2 * (pair % 2) + odd // 2)
+                b, ft, side = piece(tick, LAG_ACTIVATE)
+                if 0 <= b < B:
+                    activate(b, ft, side)
+                if 0 <= piece(tick, LAG_DEVIATION)[0] < B and piece(tick, LAG_DEVIATION)[1:] == (0, 0):
+                    deviation(piece(tick, LAG_DEVIATION)[0])
+                if 0 <= piece(tick, LAG_FACTORS)[0] < B and piece(tick, LAG_FACTORS)[1:] == (0, 0):
+                    factors(piece(tick, LAG_FACTORS)[0])
+                b, side, ft = piece(tick, LAG_NORMALISE)
+                if 0 <= b < B:
+                    normalise(b, side, ft)
+                b, side, first = piece(tick, LAG_REGROUP)
+                if 0 <= b < B and first == 0:
+                    regroup(b, side)
+                b, side, first = piece(tick, LAG_QUANTISE)
+                if 0 <= b < B and first == 0:
+                    quantise(b, side)

@@ -157,7 +157,6 @@ def tile_multiheadselfattention_pa_t_kernel(
                     stat_pool.tile([P, STATS], F32, name="sum_p", tag="sum_p"),
                     stat_pool.tile([P, STATS], F32, name="sum_pp", tag="sum_pp"),
                 )
-            sum_p, sum_pp = sums[b]
             col = ft * SIDES + side
             vals = acts[b][:, ft, side].rearrange("p j r -> p (j r)")
             nc.vector.scalar_tensor_tensor(
@@ -167,10 +166,18 @@ def tile_multiheadselfattention_pa_t_kernel(
                 in1=vals,
                 op0=ALU.mult,
                 op1=ALU.max,
-                accum_out=sum_p[:, col : col + 1],
+                accum_out=sums[b][0][:, col : col + 1],
             )
+
+        def sum_squares(b, ft, side):
+            col = ft * SIDES + side
             squares = junk_pool.tile([P, K], BF16, tag="squares")
-            nc.scalar.activation(out=squares[:], in_=vals, func=ACT.Square, accum_out=sum_pp[:, col : col + 1])
+            nc.scalar.activation(
+                out=squares[:],
+                in_=acts[b][:, ft, side].rearrange("p j r -> p (j r)"),
+                func=ACT.Square,
+                accum_out=sums[b][1][:, col : col + 1],
+            )
 
         def deviation(b):
             sum_p, sum_pp = sums[b]
@@ -207,23 +214,14 @@ def tile_multiheadselfattention_pa_t_kernel(
             factor, offset = norms[b]
             col = ft * SIDES + side
             vals = acts[b][:, ft, side].rearrange("p j r -> p (j r)")
-            if ft % 2 == 0:
-                nc.vector.tensor_scalar(
-                    out=vals,
-                    in0=vals,
-                    scalar1=factor[:, col : col + 1],
-                    scalar2=offset[:, col : col + 1],
-                    op0=ALU.mult,
-                    op1=ALU.add,
-                )
-            else:
-                nc.scalar.activation(
-                    out=vals,
-                    in_=vals,
-                    func=ACT.Identity,
-                    scale=factor[:, col : col + 1],
-                    bias=offset[:, col : col + 1],
-                )
+            nc.gpsimd.tensor_scalar(
+                out=vals,
+                in0=vals,
+                scalar1=factor[:, col : col + 1],
+                scalar2=offset[:, col : col + 1],
+                op0=ALU.mult,
+                op1=ALU.add,
+            )
 
         def flip(b, side, j):
             flipped = flip_psum.tile([P, T], F32, tag="flip")
@@ -293,12 +291,13 @@ def tile_multiheadselfattention_pa_t_kernel(
 
         TICKS = FRAME_TILES * PACK
         LAG_ACTIVATE = 4
-        LAG_DEVIATION = LAG_ACTIVATE + TICKS + 1
+        LAG_SQUARES = LAG_ACTIVATE + 1
+        LAG_DEVIATION = LAG_SQUARES + TICKS
         LAG_FACTORS = LAG_DEVIATION + 1
-        LAG_NORMALISE = LAG_FACTORS + 1
+        LAG_NORMALISE = LAG_FACTORS + 2
         LAG_FLIP = LAG_NORMALISE + 5
         LAG_GAIN = LAG_FLIP + 1
-        LAG_REGROUP = LAG_GAIN + 4
+        LAG_REGROUP = LAG_GAIN + 5
         LAG_QUANTISE = LAG_REGROUP + 2
         LAG_SCORE = LAG_QUANTISE + 6
         LAG_STORE = LAG_SCORE + 1
@@ -327,10 +326,15 @@ def tile_multiheadselfattention_pa_t_kernel(
                 b, ft, side = piece(tick, LAG_ACTIVATE)
                 if 0 <= b < B:
                     activate(b, ft, side)
-                if 0 <= piece(tick, LAG_DEVIATION)[0] < B and piece(tick, LAG_DEVIATION)[1:] == (0, 0):
-                    deviation(piece(tick, LAG_DEVIATION)[0])
-                if 0 <= piece(tick, LAG_FACTORS)[0] < B and piece(tick, LAG_FACTORS)[1:] == (0, 0):
-                    factors(piece(tick, LAG_FACTORS)[0])
+                b, ft, side = piece(tick, LAG_SQUARES)
+                if 0 <= b < B:
+                    sum_squares(b, ft, side)
+                b, first, second = piece(tick, LAG_DEVIATION)
+                if 0 <= b < B and first == 0 and second == 0:
+                    deviation(b)
+                b, first, second = piece(tick, LAG_FACTORS)
+                if 0 <= b < B and first == 0 and second == 0:
+                    factors(b)
                 b, side, ft = piece(tick, LAG_NORMALISE)
                 if 0 <= b < B:
                     normalise(b, side, ft)

@@ -32,7 +32,7 @@ def tile_multiheadselfattention_pa_t_kernel(
     nc = tc.nc
     with ExitStack() as ctx:
         const = ctx.enter_context(tc.tile_pool(name="const", bufs=1))
-        x_pool = ctx.enter_context(tc.tile_pool(name="x", bufs=1))
+        x_pool = ctx.enter_context(tc.tile_pool(name="x", bufs=3))
         act_pool = ctx.enter_context(tc.tile_pool(name="act", bufs=3))
         junk_pool = ctx.enter_context(tc.tile_pool(name="junk", bufs=4))
         stat_pool = ctx.enter_context(tc.tile_pool(name="stat", bufs=2))
@@ -59,14 +59,6 @@ def tile_multiheadselfattention_pa_t_kernel(
         nc.scalar.dma_start(out=gs_raw[2:4, :], in_=lwk.rearrange("h d f -> h (d f)"))
         nc.scalar.dma_start(out=gs_raw[4:6, :], in_=lbq.rearrange("h d f -> h (d f)"))
         nc.scalar.dma_start(out=gs_raw[6:8, :], in_=lbk.rearrange("h d f -> h (d f)"))
-
-        x_sb = []
-        for b in range(B):
-            x_b = x_pool.tile([P, T, F], BF16, name="x_b%d" % b)
-            for ft in range(FRAME_TILES):
-                frames = slice(ft * P, (ft + 1) * P)
-                nc.sync.dma_start(out=x_b[:, frames, :], in_=x[b, :, frames, :])
-            x_sb.append(x_b)
 
         ident = const.tile([P, P], F32)
         make_identity(nc, ident[:])
@@ -122,6 +114,8 @@ def tile_multiheadselfattention_pa_t_kernel(
             out=gain_shift[:], in_=gs_flip[:].rearrange("p (j r) -> p j r", j=PACK)[:, :, 0 : 2 * SIDES]
         )
 
+        x_raw = {}
+        x_by_f = {}
         acts = {}
         sums = {}
         norms = {}
@@ -132,6 +126,25 @@ def tile_multiheadselfattention_pa_t_kernel(
         score_banks = {}
         results = {}
 
+        def load(b):
+            x_raw[b] = x_pool.tile([P, T, F], BF16, name="x_raw", tag="x_raw")
+            for ft in range(FRAME_TILES):
+                frames = slice(ft * P, (ft + 1) * P)
+                nc.sync.dma_start(out=x_raw[b][:, frames, :], in_=x[b, :, frames, :])
+
+        def sort_by_frequency(b, ft):
+            if ft == 0:
+                x_by_f[b] = x_pool.tile([P, F, T], BF16, name="x_by_f", tag="x_by_f")
+            frames = slice(ft * P, (ft + 1) * P)
+            nc.gpsimd.tensor_scalar(
+                out=x_by_f[b][:, :, frames],
+                in0=x_raw[b][:, frames, :].rearrange("c t f -> c f t"),
+                scalar1=1.0,
+                scalar2=0.0,
+                op0=ALU.mult,
+                op1=ALU.add,
+            )
+
         def convolve(b, ft, j):
             if ft == 0 and j == 0:
                 acts[b] = act_pool.tile([P, FRAME_TILES, SIDES, PACK, P], F32, name="act", tag="act")
@@ -139,7 +152,7 @@ def tile_multiheadselfattention_pa_t_kernel(
             for fh in range(F_HI):
                 nc.tensor.matmul(
                     out=bank[:, :, fh, :],
-                    lhsT=x_sb[b][:, ft * P : (ft + 1) * P, fh * PACK + j],
+                    lhsT=x_by_f[b][:, fh * PACK + j, ft * P : (ft + 1) * P],
                     rhs=w_t[:].rearrange("c (g dl) -> c g dl", dl=PACK),
                     start=True,
                     stop=True,
@@ -214,14 +227,23 @@ def tile_multiheadselfattention_pa_t_kernel(
             factor, offset = norms[b]
             col = ft * SIDES + side
             vals = acts[b][:, ft, side].rearrange("p j r -> p (j r)")
-            nc.gpsimd.tensor_scalar(
-                out=vals,
-                in0=vals,
-                scalar1=factor[:, col : col + 1],
-                scalar2=offset[:, col : col + 1],
-                op0=ALU.mult,
-                op1=ALU.add,
-            )
+            if ft % 2 == 0:
+                nc.vector.tensor_scalar(
+                    out=vals,
+                    in0=vals,
+                    scalar1=factor[:, col : col + 1],
+                    scalar2=offset[:, col : col + 1],
+                    op0=ALU.mult,
+                    op1=ALU.add,
+                )
+            else:
+                nc.scalar.activation(
+                    out=vals,
+                    in_=vals,
+                    func=ACT.Identity,
+                    scale=factor[:, col : col + 1],
+                    bias=offset[:, col : col + 1],
+                )
 
         def flip(b, side, j):
             flipped = flip_psum.tile([P, T], F32, tag="flip")
@@ -287,10 +309,11 @@ def tile_multiheadselfattention_pa_t_kernel(
                 out=result[:, ft, :], in_=score_banks[(b, h, ft)][:], func=ACT.Copy, scale=1.0 / math.sqrt(K)
             )
             if ft == FRAME_TILES - 1:
-                nc.sync.dma_start(out=out[b, h].rearrange("(ft p) s -> p ft s", p=P), in_=result[:])
+                nc.scalar.dma_start(out=out[b, h].rearrange("(ft p) s -> p ft s", p=P), in_=result[:])
 
         TICKS = FRAME_TILES * PACK
-        LAG_ACTIVATE = 4
+        LAG_CONVOLVE = 8
+        LAG_ACTIVATE = LAG_CONVOLVE + 4
         LAG_SQUARES = LAG_ACTIVATE + 1
         LAG_DEVIATION = LAG_SQUARES + TICKS
         LAG_FACTORS = LAG_DEVIATION + 1
@@ -306,9 +329,17 @@ def tile_multiheadselfattention_pa_t_kernel(
             b, rest = divmod(tick - lag, TICKS)
             return (b,) + divmod(rest, 4)
 
+        X_AHEAD = 3
         with tc.manual_schedule():
+            for b in range(X_AHEAD):
+                load(b)
             for tick in range(B * TICKS + LAG_STORE):
-                b, ft, j = piece(tick, 0)
+                b, ft, first = piece(tick, 0)
+                if 0 <= b < B and first == 0:
+                    sort_by_frequency(b, ft)
+                    if ft == FRAME_TILES - 1 and b + X_AHEAD < B:
+                        load(b + X_AHEAD)
+                b, ft, j = piece(tick, LAG_CONVOLVE)
                 if 0 <= b < B:
                     convolve(b, ft, j)
                 b, side, j = piece(tick, LAG_FLIP)

@@ -32,13 +32,13 @@ def tile_multiheadselfattention_pa_t_kernel(
     nc = tc.nc
     with ExitStack() as ctx:
         const = ctx.enter_context(tc.tile_pool(name="const", bufs=1))
-        x_pool = ctx.enter_context(tc.tile_pool(name="x", bufs=3))
+        x_pool = ctx.enter_context(tc.tile_pool(name="x", bufs=1))
         act_pool = ctx.enter_context(tc.tile_pool(name="act", bufs=3))
         junk_pool = ctx.enter_context(tc.tile_pool(name="junk", bufs=4))
         stat_pool = ctx.enter_context(tc.tile_pool(name="stat", bufs=2))
         plane_pool = ctx.enter_context(tc.tile_pool(name="plane", bufs=2))
         code_pool = ctx.enter_context(tc.tile_pool(name="code", bufs=2))
-        store_pool = ctx.enter_context(tc.tile_pool(name="store", bufs=2))
+        store_pool = ctx.enter_context(tc.tile_pool(name="store", bufs=4))
         conv_psum = ctx.enter_context(tc.psum_pool(name="conv_psum", bufs=3))
         flip_psum = ctx.enter_context(tc.psum_pool(name="flip_psum", bufs=3))
         score_psum = ctx.enter_context(tc.psum_pool(name="score_psum", bufs=2))
@@ -59,6 +59,14 @@ def tile_multiheadselfattention_pa_t_kernel(
         nc.scalar.dma_start(out=gs_raw[2:4, :], in_=lwk.rearrange("h d f -> h (d f)"))
         nc.scalar.dma_start(out=gs_raw[4:6, :], in_=lbq.rearrange("h d f -> h (d f)"))
         nc.scalar.dma_start(out=gs_raw[6:8, :], in_=lbk.rearrange("h d f -> h (d f)"))
+
+        x_sb = []
+        for b in range(B):
+            x_b = x_pool.tile([P, T, F], BF16, name="x_b%d" % b)
+            for ft in range(FRAME_TILES):
+                frames = slice(ft * P, (ft + 1) * P)
+                nc.sync.dma_start(out=x_b[:, frames, :], in_=x[b, :, frames, :])
+            x_sb.append(x_b)
 
         ident = const.tile([P, P], F32)
         make_identity(nc, ident[:])
@@ -114,8 +122,6 @@ def tile_multiheadselfattention_pa_t_kernel(
             out=gain_shift[:], in_=gs_flip[:].rearrange("p (j r) -> p j r", j=PACK)[:, :, 0 : 2 * SIDES]
         )
 
-        x_raw = {}
-        x_by_f = {}
         acts = {}
         sums = {}
         norms = {}
@@ -124,26 +130,6 @@ def tile_multiheadselfattention_pa_t_kernel(
         grouped_of = {}
         mx_ops = {}
         score_banks = {}
-        results = {}
-
-        def load(b):
-            x_raw[b] = x_pool.tile([P, T, F], BF16, name="x_raw", tag="x_raw")
-            for ft in range(FRAME_TILES):
-                frames = slice(ft * P, (ft + 1) * P)
-                nc.sync.dma_start(out=x_raw[b][:, frames, :], in_=x[b, :, frames, :])
-
-        def sort_by_frequency(b, ft):
-            if ft == 0:
-                x_by_f[b] = x_pool.tile([P, F, T], BF16, name="x_by_f", tag="x_by_f")
-            frames = slice(ft * P, (ft + 1) * P)
-            nc.gpsimd.tensor_scalar(
-                out=x_by_f[b][:, :, frames],
-                in0=x_raw[b][:, frames, :].rearrange("c t f -> c f t"),
-                scalar1=1.0,
-                scalar2=0.0,
-                op0=ALU.mult,
-                op1=ALU.add,
-            )
 
         def convolve(b, ft, j):
             if ft == 0 and j == 0:
@@ -152,7 +138,7 @@ def tile_multiheadselfattention_pa_t_kernel(
             for fh in range(F_HI):
                 nc.tensor.matmul(
                     out=bank[:, :, fh, :],
-                    lhsT=x_by_f[b][:, fh * PACK + j, ft * P : (ft + 1) * P],
+                    lhsT=x_sb[b][:, ft * P : (ft + 1) * P, fh * PACK + j],
                     rhs=w_t[:].rearrange("c (g dl) -> c g dl", dl=PACK),
                     start=True,
                     stop=True,
@@ -227,7 +213,7 @@ def tile_multiheadselfattention_pa_t_kernel(
             factor, offset = norms[b]
             col = ft * SIDES + side
             vals = acts[b][:, ft, side].rearrange("p j r -> p (j r)")
-            if ft % 2 == 0:
+            if (side * FRAME_TILES + ft) % 3 != 0:
                 nc.vector.tensor_scalar(
                     out=vals,
                     in0=vals,
@@ -302,18 +288,14 @@ def tile_multiheadselfattention_pa_t_kernel(
             score_banks[(b, h, ft)] = bank
 
         def scale_and_store(b, h, ft):
-            if ft == 0:
-                results[(b, h)] = store_pool.tile([P, FRAME_TILES, T], F32, name="result", tag="result")
-            result = results[(b, h)]
+            result = store_pool.tile([P, T], F32, tag="result")
             nc.scalar.activation(
-                out=result[:, ft, :], in_=score_banks[(b, h, ft)][:], func=ACT.Copy, scale=1.0 / math.sqrt(K)
+                out=result[:], in_=score_banks[(b, h, ft)][:], func=ACT.Copy, scale=1.0 / math.sqrt(K)
             )
-            if ft == FRAME_TILES - 1:
-                nc.scalar.dma_start(out=out[b, h].rearrange("(ft p) s -> p ft s", p=P), in_=result[:])
+            nc.sync.dma_start(out=out[b, h, ft * P : (ft + 1) * P, :], in_=result[:])
 
         TICKS = FRAME_TILES * PACK
-        LAG_CONVOLVE = 8
-        LAG_ACTIVATE = LAG_CONVOLVE + 4
+        LAG_ACTIVATE = 4
         LAG_SQUARES = LAG_ACTIVATE + 1
         LAG_DEVIATION = LAG_SQUARES + TICKS
         LAG_FACTORS = LAG_DEVIATION + 1
@@ -329,49 +311,40 @@ def tile_multiheadselfattention_pa_t_kernel(
             b, rest = divmod(tick - lag, TICKS)
             return (b,) + divmod(rest, 4)
 
-        X_AHEAD = 3
-        with tc.manual_schedule():
-            for b in range(X_AHEAD):
-                load(b)
-            for tick in range(B * TICKS + LAG_STORE):
-                b, ft, first = piece(tick, 0)
-                if 0 <= b < B and first == 0:
-                    sort_by_frequency(b, ft)
-                    if ft == FRAME_TILES - 1 and b + X_AHEAD < B:
-                        load(b + X_AHEAD)
-                b, ft, j = piece(tick, LAG_CONVOLVE)
-                if 0 <= b < B:
-                    convolve(b, ft, j)
-                b, side, j = piece(tick, LAG_FLIP)
-                if 0 <= b < B:
-                    flip(b, side, j)
-                b, pair, odd = piece(tick, LAG_SCORE)
-                if 0 <= b < B and odd % 2 == 0:
-                    score(b, pair // 2, 2 * (pair % 2) + odd // 2)
-                b, side, j = piece(tick, LAG_GAIN)
-                if 0 <= b < B:
-                    gain_and_shift(b, side, j)
-                b, pair, odd = piece(tick, LAG_STORE)
-                if 0 <= b < B and odd % 2 == 0:
-                    scale_and_store(b, pair // 2, 2 * (pair % 2) + odd // 2)
-                b, ft, side = piece(tick, LAG_ACTIVATE)
-                if 0 <= b < B:
-                    activate(b, ft, side)
-                b, ft, side = piece(tick, LAG_SQUARES)
-                if 0 <= b < B:
-                    sum_squares(b, ft, side)
-                b, first, second = piece(tick, LAG_DEVIATION)
-                if 0 <= b < B and first == 0 and second == 0:
-                    deviation(b)
-                b, first, second = piece(tick, LAG_FACTORS)
-                if 0 <= b < B and first == 0 and second == 0:
-                    factors(b)
-                b, side, ft = piece(tick, LAG_NORMALISE)
-                if 0 <= b < B:
-                    normalise(b, side, ft)
-                b, side, first = piece(tick, LAG_REGROUP)
-                if 0 <= b < B and first == 0:
-                    regroup(b, side)
-                b, side, first = piece(tick, LAG_QUANTISE)
-                if 0 <= b < B and first == 0:
-                    quantise(b, side)
+        for tick in range(B * TICKS + LAG_STORE):
+            b, ft, j = piece(tick, 0)
+            if 0 <= b < B:
+                convolve(b, ft, j)
+            b, side, j = piece(tick, LAG_FLIP)
+            if 0 <= b < B:
+                flip(b, side, j)
+            b, pair, odd = piece(tick, LAG_SCORE)
+            if 0 <= b < B and odd % 2 == 0:
+                score(b, pair // 2, 2 * (pair % 2) + odd // 2)
+            b, side, j = piece(tick, LAG_GAIN)
+            if 0 <= b < B:
+                gain_and_shift(b, side, j)
+            b, pair, odd = piece(tick, LAG_STORE)
+            if 0 <= b < B and odd % 2 == 0:
+                scale_and_store(b, pair // 2, 2 * (pair % 2) + odd // 2)
+            b, ft, side = piece(tick, LAG_ACTIVATE)
+            if 0 <= b < B:
+                activate(b, ft, side)
+            b, ft, side = piece(tick, LAG_SQUARES)
+            if 0 <= b < B:
+                sum_squares(b, ft, side)
+            b, first, second = piece(tick, LAG_DEVIATION)
+            if 0 <= b < B and first == 0 and second == 0:
+                deviation(b)
+            b, first, second = piece(tick, LAG_FACTORS)
+            if 0 <= b < B and first == 0 and second == 0:
+                factors(b)
+            b, side, ft = piece(tick, LAG_NORMALISE)
+            if 0 <= b < B:
+                normalise(b, side, ft)
+            b, side, first = piece(tick, LAG_REGROUP)
+            if 0 <= b < B and first == 0:
+                regroup(b, side)
+            b, side, first = piece(tick, LAG_QUANTISE)
+            if 0 <= b < B and first == 0:
+                quantise(b, side)

@@ -121,9 +121,17 @@ def tile_multiheadselfattention_pa_t_kernel(
         nc.vector.tensor_copy(
             out=gain_shift[:], in_=gs_flip[:].rearrange("p (j r) -> p j r", j=PACK)[:, :, 0 : 2 * SIDES]
         )
+        for side in range(SIDES):
+            h, qk = divmod(side, 2)
+            nc.vector.tensor_scalar_mul(
+                out=gain_shift[:, :, qk * H + h],
+                in0=gain_shift[:, :, qk * H + h],
+                scalar1=sign[:, side : side + 1],
+            )
 
         acts = {}
         sums = {}
+        stds = {}
         norms = {}
         flips = {}
         planes_of = {}
@@ -180,32 +188,22 @@ def tile_multiheadselfattention_pa_t_kernel(
 
         def deviation(b):
             sum_p, sum_pp = sums[b]
-            mean = stat_pool.tile([P, STATS], F32, tag="mean")
-            nc.vector.tensor_scalar_mul(out=mean[:], in0=sum_p[:], scalar1=1.0 / K)
             mean_sq = stat_pool.tile([P, STATS], F32, tag="mean_sq")
-            nc.vector.tensor_tensor(out=mean_sq[:], in0=mean[:], in1=mean[:], op=ALU.mult)
+            nc.scalar.activation(out=mean_sq[:], in_=sum_p[:], func=ACT.Square, scale=1.0 / K)
             var = stat_pool.tile([P, STATS], F32, tag="var")
             nc.vector.scalar_tensor_tensor(
                 out=var[:], in0=sum_pp[:], scalar=1.0 / K, in1=mean_sq[:], op0=ALU.mult, op1=ALU.subtract
             )
             std = stat_pool.tile([P, STATS], F32, tag="std")
             nc.scalar.activation(out=std[:], in_=var[:], func=ACT.Sqrt, bias=eps_col[:, 0:1])
-            norms[b] = (mean, std)
+            stds[b] = std
 
         def factors(b):
-            mean, std = norms[b]
-            rstd = stat_pool.tile([P, STATS], F32, tag="rstd")
-            nc.vector.reciprocal(out=rstd[:], in_=std[:])
             factor = stat_pool.tile([P, STATS], F32, tag="factor")
-            nc.vector.tensor_tensor(
-                out=factor[:].rearrange("p (ft s) -> p ft s", s=SIDES),
-                in0=rstd[:].rearrange("p (ft s) -> p ft s", s=SIDES),
-                in1=sign[:].unsqueeze(1).to_broadcast([P, FRAME_TILES, SIDES]),
-                op=ALU.mult,
-            )
+            nc.vector.reciprocal(out=factor[:], in_=stds[b][:])
             offset = stat_pool.tile([P, STATS], F32, tag="offset")
             nc.vector.scalar_tensor_tensor(
-                out=offset[:], in0=mean[:], scalar=-1.0, in1=factor[:], op0=ALU.mult, op1=ALU.mult
+                out=offset[:], in0=sums[b][0][:], scalar=-1.0 / K, in1=factor[:], op0=ALU.mult, op1=ALU.mult
             )
             norms[b] = (factor, offset)
 
@@ -213,7 +211,7 @@ def tile_multiheadselfattention_pa_t_kernel(
             factor, offset = norms[b]
             col = ft * SIDES + side
             vals = acts[b][:, ft, side].rearrange("p j r -> p (j r)")
-            if (side * FRAME_TILES + ft) % 3 != 0:
+            if b == B - 1 or (b > 0 and (side * FRAME_TILES + ft) % 3 != 0):
                 nc.vector.tensor_scalar(
                     out=vals,
                     in0=vals,
@@ -243,13 +241,15 @@ def tile_multiheadselfattention_pa_t_kernel(
             if j == 0:
                 planes_of[(b, side)] = plane_pool.tile([P, PACK, T], BF16, name="planes", tag="planes")
             h, qk = divmod(side, 2)
-            nc.scalar.activation(
-                out=planes_of[(b, side)][:, j, :],
-                in_=flips[(b, side, j)][:],
-                func=ACT.Identity,
-                scale=gain_shift[:, j, qk * H + h : qk * H + h + 1],
-                bias=gain_shift[:, j, SIDES + qk * H + h : SIDES + qk * H + h + 1],
-            )
+            gain = gain_shift[:, j, qk * H + h : qk * H + h + 1]
+            shift = gain_shift[:, j, SIDES + qk * H + h : SIDES + qk * H + h + 1]
+            plane = planes_of[(b, side)][:, j, :]
+            if b == B - 1 and j % 2 == 1:
+                nc.vector.tensor_scalar(
+                    out=plane, in0=flips[(b, side, j)][:], scalar1=gain, scalar2=shift, op0=ALU.mult, op1=ALU.add
+                )
+            else:
+                nc.scalar.activation(out=plane, in_=flips[(b, side, j)][:], func=ACT.Identity, scale=gain, bias=shift)
 
         def regroup(b, side):
             grouped = plane_pool.tile([P, T, PACK], BF16, tag="grouped", align_bytes=64)
@@ -289,9 +289,12 @@ def tile_multiheadselfattention_pa_t_kernel(
 
         def scale_and_store(b, h, ft):
             result = store_pool.tile([P, T], F32, tag="result")
-            nc.scalar.activation(
-                out=result[:], in_=score_banks[(b, h, ft)][:], func=ACT.Copy, scale=1.0 / math.sqrt(K)
-            )
+            if b == B - 1 and ft % 2 == 1:
+                nc.vector.tensor_scalar_mul(out=result[:], in0=score_banks[(b, h, ft)][:], scalar1=1.0 / math.sqrt(K))
+            else:
+                nc.scalar.activation(
+                    out=result[:], in_=score_banks[(b, h, ft)][:], func=ACT.Copy, scale=1.0 / math.sqrt(K)
+                )
             nc.sync.dma_start(out=out[b, h, ft * P : (ft + 1) * P, :], in_=result[:])
 
         TICKS = FRAME_TILES * PACK

@@ -22,6 +22,9 @@ SIDES = 2 * H
 F_HI = F // PACK
 D_HI = D // PACK
 STATS = FRAME_TILES * SIDES
+LAST = B - 1
+RUN = 4
+SCALAR_EVERY = 3
 
 FLOPS = 2 * (2 * H * D) * C * (B * T * F) + 2 * B * H * T * T * K
 
@@ -107,6 +110,14 @@ def tile_multiheadselfattention_pa_t_kernel(
                 scalar1=sign[:, side : side + 1],
             )
 
+        bias_flip = flip_psum.tile([P, T], F32, tag="flip")
+        bias_flat = bias_t[:].rearrange("p s dh fh dl -> p (s dh fh dl)")
+        for block in range(SIDES):
+            cols = slice(block * P, (block + 1) * P)
+            nc.tensor.transpose(out=bias_flip[:, cols], in_=bias_flat[:, cols], identity=ident[:])
+        bias_cols = const.tile([P, SIDES, P], F32)
+        nc.vector.tensor_copy(out=bias_cols[:].rearrange("p s t -> p (s t)"), in_=bias_flip[:])
+
         gs_rows = const.tile([P, PACK, D_HI, F_HI, PACK], F32)
         gs_view = gs_raw[:].rearrange("p (dh dl fh j) -> p j dh fh dl", dl=PACK, fh=F_HI, j=PACK)
         gs_flip = flip_psum.tile([P, T], F32, tag="flip")
@@ -139,24 +150,35 @@ def tile_multiheadselfattention_pa_t_kernel(
         mx_ops = {}
         score_banks = {}
 
+        def vector_empties(b, bank_number):
+            return b == LAST and bank_number % 2 == 1
+
         def convolve(b, ft, j):
             if ft == 0 and j == 0:
                 acts[b] = act_pool.tile([P, FRAME_TILES, SIDES, PACK, P], F32, name="act", tag="act")
             bank = conv_psum.tile([P, SIDES * D_HI, F_HI, PACK], F32, tag="conv")
+            by_side = bank[:].rearrange("p (s dh) fh dl -> p s (dh fh dl)", s=SIDES)
+            for side in range(SIDES):
+                nc.tensor.matmul(
+                    out=by_side[:, side, :],
+                    lhsT=bias_cols[:, side, :],
+                    rhs=ident[:],
+                    is_transpose=True,
+                    start=(side == 0),
+                    stop=False,
+                )
             for fh in range(F_HI):
                 nc.tensor.matmul(
                     out=bank[:, :, fh, :],
                     lhsT=x_sb[b][:, ft * P : (ft + 1) * P, fh * PACK + j],
                     rhs=w_t[:].rearrange("c (g dl) -> c g dl", dl=PACK),
-                    start=True,
-                    stop=True,
+                    start=False,
+                    stop=(fh == F_HI - 1),
                 )
-            nc.vector.tensor_tensor(
-                out=acts[b][:, ft, :, j, :],
-                in0=bank[:].rearrange("p (s dh) fh dl -> p s (dh fh dl)", s=SIDES),
-                in1=bias_t[:].rearrange("p s dh fh dl -> p s (dh fh dl)"),
-                op=ALU.add,
-            )
+            if (ft * PACK + j) % SCALAR_EVERY == 0:
+                nc.scalar.copy(out=acts[b][:, ft, :, j, :], in_=by_side)
+            else:
+                nc.vector.tensor_copy(out=acts[b][:, ft, :, j, :], in_=by_side)
 
         def activate(b, ft, side):
             if ft == 0 and side == 0:
@@ -211,23 +233,14 @@ def tile_multiheadselfattention_pa_t_kernel(
             factor, offset = norms[b]
             col = ft * SIDES + side
             vals = acts[b][:, ft, side].rearrange("p j r -> p (j r)")
-            if b == B - 1 or (b > 0 and (side * FRAME_TILES + ft) % 3 != 0):
-                nc.vector.tensor_scalar(
-                    out=vals,
-                    in0=vals,
-                    scalar1=factor[:, col : col + 1],
-                    scalar2=offset[:, col : col + 1],
-                    op0=ALU.mult,
-                    op1=ALU.add,
-                )
-            else:
-                nc.scalar.activation(
-                    out=vals,
-                    in_=vals,
-                    func=ACT.Identity,
-                    scale=factor[:, col : col + 1],
-                    bias=offset[:, col : col + 1],
-                )
+            nc.vector.tensor_scalar(
+                out=vals,
+                in0=vals,
+                scalar1=factor[:, col : col + 1],
+                scalar2=offset[:, col : col + 1],
+                op0=ALU.mult,
+                op1=ALU.add,
+            )
 
         def flip(b, side, j):
             flipped = flip_psum.tile([P, T], F32, tag="flip")
@@ -244,7 +257,7 @@ def tile_multiheadselfattention_pa_t_kernel(
             gain = gain_shift[:, j, qk * H + h : qk * H + h + 1]
             shift = gain_shift[:, j, SIDES + qk * H + h : SIDES + qk * H + h + 1]
             plane = planes_of[(b, side)][:, j, :]
-            if b == B - 1 and j % 2 == 1:
+            if vector_empties(b, j):
                 nc.vector.tensor_scalar(
                     out=plane, in0=flips[(b, side, j)][:], scalar1=gain, scalar2=shift, op0=ALU.mult, op1=ALU.add
                 )
@@ -254,8 +267,8 @@ def tile_multiheadselfattention_pa_t_kernel(
         def regroup(b, side):
             grouped = plane_pool.tile([P, T, PACK], BF16, tag="grouped", align_bytes=64)
             nc.vector.tensor_copy(
-                out=grouped[:].rearrange("p (c i) j -> p c j i", i=4),
-                in_=planes_of[(b, side)][:].rearrange("p j (c i) -> p c j i", i=4),
+                out=grouped[:].rearrange("p (c i) j -> p c j i", i=RUN),
+                in_=planes_of[(b, side)][:].rearrange("p j (c i) -> p c j i", i=RUN),
             )
             grouped_of[(b, side)] = grouped
 
@@ -289,7 +302,7 @@ def tile_multiheadselfattention_pa_t_kernel(
 
         def scale_and_store(b, h, ft):
             result = store_pool.tile([P, T], F32, tag="result")
-            if b == B - 1 and ft % 2 == 1:
+            if vector_empties(b, ft):
                 nc.vector.tensor_scalar_mul(out=result[:], in0=score_banks[(b, h, ft)][:], scalar1=1.0 / math.sqrt(K))
             else:
                 nc.scalar.activation(
@@ -321,33 +334,33 @@ def tile_multiheadselfattention_pa_t_kernel(
             b, side, j = piece(tick, LAG_FLIP)
             if 0 <= b < B:
                 flip(b, side, j)
-            b, pair, odd = piece(tick, LAG_SCORE)
-            if 0 <= b < B and odd % 2 == 0:
-                score(b, pair // 2, 2 * (pair % 2) + odd // 2)
+            b, outer, inner = piece(tick, LAG_SCORE)
+            if 0 <= b < B and inner % 2 == 0:
+                score(b, *divmod(2 * outer + inner // 2, FRAME_TILES))
             b, side, j = piece(tick, LAG_GAIN)
             if 0 <= b < B:
                 gain_and_shift(b, side, j)
-            b, pair, odd = piece(tick, LAG_STORE)
-            if 0 <= b < B and odd % 2 == 0:
-                scale_and_store(b, pair // 2, 2 * (pair % 2) + odd // 2)
+            b, outer, inner = piece(tick, LAG_STORE)
+            if 0 <= b < B and inner % 2 == 0:
+                scale_and_store(b, *divmod(2 * outer + inner // 2, FRAME_TILES))
             b, ft, side = piece(tick, LAG_ACTIVATE)
             if 0 <= b < B:
                 activate(b, ft, side)
             b, ft, side = piece(tick, LAG_SQUARES)
             if 0 <= b < B:
                 sum_squares(b, ft, side)
-            b, first, second = piece(tick, LAG_DEVIATION)
-            if 0 <= b < B and first == 0 and second == 0:
+            b, outer, inner = piece(tick, LAG_DEVIATION)
+            if 0 <= b < B and outer == 0 and inner == 0:
                 deviation(b)
-            b, first, second = piece(tick, LAG_FACTORS)
-            if 0 <= b < B and first == 0 and second == 0:
+            b, outer, inner = piece(tick, LAG_FACTORS)
+            if 0 <= b < B and outer == 0 and inner == 0:
                 factors(b)
             b, side, ft = piece(tick, LAG_NORMALISE)
             if 0 <= b < B:
                 normalise(b, side, ft)
-            b, side, first = piece(tick, LAG_REGROUP)
-            if 0 <= b < B and first == 0:
+            b, side, inner = piece(tick, LAG_REGROUP)
+            if 0 <= b < B and inner == 0:
                 regroup(b, side)
-            b, side, first = piece(tick, LAG_QUANTISE)
-            if 0 <= b < B and first == 0:
+            b, side, inner = piece(tick, LAG_QUANTISE)
+            if 0 <= b < B and inner == 0:
                 quantise(b, side)

@@ -24,6 +24,8 @@ D_HI = D // PACK
 STATS = FRAME_TILES * SIDES
 LAST = B - 1
 RUN = 4
+AQ_AT, AK_AT, BQ_AT, BK_AT = 0, 16, 32, 32 + H * D
+ROW_WIDTH = BK_AT + H * D
 SCALAR_EVERY = 3
 
 FLOPS = 2 * (2 * H * D) * C * (B * T * F) + 2 * B * H * T * T * K
@@ -49,13 +51,12 @@ def tile_multiheadselfattention_pa_t_kernel(
         w_raw = const.tile([P, 2, C], BF16)
         nc.scalar.dma_start(out=w_raw[:, 0, :], in_=Wq.rearrange("h d c -> (h d) c"))
         nc.scalar.dma_start(out=w_raw[:, 1, :], in_=Wk.rearrange("h d c -> (h d) c"))
-        aq_raw = const.tile([P, H], BF16)
-        ak_raw = const.tile([P, H], BF16)
-        nc.scalar.dma_start(out=aq_raw[:], in_=aq.partition_broadcast(P))
-        nc.scalar.dma_start(out=ak_raw[:], in_=ak.partition_broadcast(P))
-        b_raw = const.tile([P, 2, H * D], BF16)
-        nc.scalar.dma_start(out=b_raw[:, 0, :], in_=bq.rearrange("h d -> (h d)").partition_broadcast(P))
-        nc.scalar.dma_start(out=b_raw[:, 1, :], in_=bk.rearrange("h d -> (h d)").partition_broadcast(P))
+        row = const.tile([P, ROW_WIDTH], BF16)
+        nc.vector.memset(row[:], 0.0)
+        nc.sync.dma_start(out=row[0:1, AQ_AT : AQ_AT + H], in_=aq.unsqueeze(0))
+        nc.sync.dma_start(out=row[0:1, AK_AT : AK_AT + H], in_=ak.unsqueeze(0))
+        nc.sync.dma_start(out=row[0:1, BQ_AT : BQ_AT + H * D], in_=bq.rearrange("h d -> (h d)").unsqueeze(0))
+        nc.sync.dma_start(out=row[0:1, BK_AT : BK_AT + H * D], in_=bk.rearrange("h d -> (h d)").unsqueeze(0))
         gs_raw = const.tile([P, K], BF16)
         nc.vector.memset(gs_raw[:], 0.0)
         nc.scalar.dma_start(out=gs_raw[0:2, :], in_=lwq.rearrange("h d f -> h (d f)"))
@@ -75,11 +76,23 @@ def tile_multiheadselfattention_pa_t_kernel(
         make_identity(nc, ident[:])
         eps_col = const.tile([P, 1], F32)
         nc.vector.memset(eps_col[:], EPS)
+        warm_col = const.tile([P, 1], F32)
+        nc.scalar.activation(out=warm_col[:], in_=eps_col[:], func=ACT.Sqrt)
+
+        ones_row = const.tile([P, P], BF16)
+        nc.vector.memset(ones_row[:], 0.0)
+        nc.vector.memset(ones_row[0:1, :], 1.0)
+        spread = flip_psum.tile([P, T], F32, tag="flip")
+        nc.tensor.matmul(out=spread[:, 0:ROW_WIDTH], lhsT=ones_row[:], rhs=row[:], start=True, stop=True)
+        b_raw = const.tile([P, 2, H * D], F32)
+        nc.vector.tensor_copy(
+            out=b_raw[:].rearrange("p qk n -> p (qk n)"), in_=spread[:, BQ_AT:ROW_WIDTH]
+        )
 
         slope = const.tile([P, SIDES], F32)
         slope_by_head = slope[:].rearrange("p (h qk) -> p h qk", qk=2)
-        nc.vector.tensor_copy(out=slope_by_head[:, :, 0], in_=aq_raw[:])
-        nc.vector.tensor_copy(out=slope_by_head[:, :, 1], in_=ak_raw[:])
+        nc.vector.tensor_copy(out=slope_by_head[:, :, 0], in_=spread[:, AQ_AT : AQ_AT + H])
+        nc.vector.tensor_copy(out=slope_by_head[:, :, 1], in_=spread[:, AK_AT : AK_AT + H])
         sign = const.tile([P, SIDES], F32)
         nc.vector.tensor_scalar(out=sign[:], in0=slope[:], scalar1=1.0, scalar2=2.0, op0=ALU.is_le, op1=ALU.mult)
         nc.vector.tensor_scalar_add(out=sign[:], in0=sign[:], scalar1=-1.0)

@@ -26,7 +26,7 @@ LAST = B - 1
 RUN = 4
 AQ_AT, AK_AT, BQ_AT, BK_AT = 0, 16, 32, 32 + H * D
 ROW_WIDTH = BK_AT + H * D
-SCALAR_EVERY = 3
+SCALAR_BANKS = 7
 
 FLOPS = 2 * (2 * H * D) * C * (B * T * F) + 2 * B * H * T * T * K
 
@@ -188,7 +188,7 @@ def tile_multiheadselfattention_pa_t_kernel(
                     start=False,
                     stop=(fh == F_HI - 1),
                 )
-            if (ft * PACK + j) % SCALAR_EVERY == 0:
+            if ((ft * PACK + j) * SCALAR_BANKS) % (FRAME_TILES * PACK) < SCALAR_BANKS:
                 nc.scalar.copy(out=acts[b][:, ft, :, j, :], in_=by_side)
             else:
                 nc.vector.tensor_copy(out=acts[b][:, ft, :, j, :], in_=by_side)

@@ -43,7 +43,7 @@ def tile_multiheadselfattention_pa_t_kernel(
         stat_pool = ctx.enter_context(tc.tile_pool(name="stat", bufs=2))
         plane_pool = ctx.enter_context(tc.tile_pool(name="plane", bufs=2))
         code_pool = ctx.enter_context(tc.tile_pool(name="code", bufs=2))
-        store_pool = ctx.enter_context(tc.tile_pool(name="store", bufs=4))
+        store_pool = ctx.enter_context(tc.tile_pool(name="store", bufs=8))
         conv_psum = ctx.enter_context(tc.psum_pool(name="conv_psum", bufs=3))
         flip_psum = ctx.enter_context(tc.psum_pool(name="flip_psum", bufs=3))
         score_psum = ctx.enter_context(tc.psum_pool(name="score_psum", bufs=2))
@@ -84,10 +84,6 @@ def tile_multiheadselfattention_pa_t_kernel(
         nc.vector.memset(ones_row[0:1, :], 1.0)
         spread = flip_psum.tile([P, T], F32, tag="flip")
         nc.tensor.matmul(out=spread[:, 0:ROW_WIDTH], lhsT=ones_row[:], rhs=row[:], start=True, stop=True)
-        b_raw = const.tile([P, 2, H * D], F32)
-        nc.vector.tensor_copy(
-            out=b_raw[:].rearrange("p qk n -> p (qk n)"), in_=spread[:, BQ_AT:ROW_WIDTH]
-        )
 
         slope = const.tile([P, SIDES], F32)
         slope_by_head = slope[:].rearrange("p (h qk) -> p h qk", qk=2)
@@ -96,6 +92,27 @@ def tile_multiheadselfattention_pa_t_kernel(
         sign = const.tile([P, SIDES], F32)
         nc.vector.tensor_scalar(out=sign[:], in0=slope[:], scalar1=1.0, scalar2=2.0, op0=ALU.is_le, op1=ALU.mult)
         nc.vector.tensor_scalar_add(out=sign[:], in0=sign[:], scalar1=-1.0)
+
+        bias_t = const.tile([P, SIDES, D_HI, F_HI, PACK], F32)
+        for side in range(SIDES):
+            h, qk = divmod(side, 2)
+            at = BQ_AT + (qk * H + h) * D
+            nc.vector.tensor_scalar_mul(
+                out=bias_t[:, side],
+                in0=spread[:, at : at + D]
+                .rearrange("p (dh dl) -> p dh dl", dl=PACK)
+                .unsqueeze(2)
+                .to_broadcast([P, D_HI, F_HI, PACK]),
+                scalar1=sign[:, side : side + 1],
+            )
+
+        bias_flip = flip_psum.tile([P, T], F32, tag="flip")
+        bias_flat = bias_t[:].rearrange("p s dh fh dl -> p (s dh fh dl)")
+        for block in range(SIDES):
+            cols = slice(block * P, (block + 1) * P)
+            nc.tensor.transpose(out=bias_flip[:, cols], in_=bias_flat[:, cols], identity=ident[:])
+        bias_col = const.tile([P, SIDES], F32)
+        nc.vector.tensor_copy(out=bias_col[:], in_=bias_flip[:].rearrange("p (s t) -> p s t", s=SIDES)[:, :, 0])
 
         w_f32 = const.tile([P, 2, C], F32)
         nc.vector.tensor_copy(out=w_f32[:], in_=w_raw[:])
@@ -110,26 +127,6 @@ def tile_multiheadselfattention_pa_t_kernel(
                 in0=w_flip[:, (qk * H + h) * D : (qk * H + h + 1) * D],
                 scalar1=sign[:, side : side + 1],
             )
-
-        bias_t = const.tile([P, SIDES, D_HI, F_HI, PACK], F32)
-        for side in range(SIDES):
-            h, qk = divmod(side, 2)
-            nc.vector.tensor_scalar_mul(
-                out=bias_t[:, side],
-                in0=b_raw[:, qk, h * D : (h + 1) * D]
-                .rearrange("p (dh dl) -> p dh dl", dl=PACK)
-                .unsqueeze(2)
-                .to_broadcast([P, D_HI, F_HI, PACK]),
-                scalar1=sign[:, side : side + 1],
-            )
-
-        bias_flip = flip_psum.tile([P, T], F32, tag="flip")
-        bias_flat = bias_t[:].rearrange("p s dh fh dl -> p (s dh fh dl)")
-        for block in range(SIDES):
-            cols = slice(block * P, (block + 1) * P)
-            nc.tensor.transpose(out=bias_flip[:, cols], in_=bias_flat[:, cols], identity=ident[:])
-        bias_cols = const.tile([P, SIDES, P], F32)
-        nc.vector.tensor_copy(out=bias_cols[:].rearrange("p s t -> p (s t)"), in_=bias_flip[:])
 
         gs_rows = const.tile([P, PACK, D_HI, F_HI, PACK], F32)
         gs_view = gs_raw[:].rearrange("p (dh dl fh j) -> p j dh fh dl", dl=PACK, fh=F_HI, j=PACK)
@@ -155,6 +152,7 @@ def tile_multiheadselfattention_pa_t_kernel(
 
         acts = {}
         sums = {}
+        variances = {}
         stds = {}
         norms = {}
         flips = {}
@@ -164,7 +162,7 @@ def tile_multiheadselfattention_pa_t_kernel(
         score_banks = {}
 
         def vector_empties(b, bank_number):
-            return b == LAST and bank_number % 2 == 1
+            return b >= LAST - 2 and bank_number % 2 == 1
 
         def convolve(b, ft, j):
             if ft == 0 and j == 0:
@@ -174,7 +172,7 @@ def tile_multiheadselfattention_pa_t_kernel(
             for side in range(SIDES):
                 nc.tensor.matmul(
                     out=by_side[:, side, :],
-                    lhsT=bias_cols[:, side, :],
+                    lhsT=bias_col[:, side : side + 1].to_broadcast([P, P]),
                     rhs=ident[:],
                     is_transpose=True,
                     start=(side == 0),
@@ -221,16 +219,21 @@ def tile_multiheadselfattention_pa_t_kernel(
                 accum_out=sums[b][1][:, col : col + 1],
             )
 
-        def deviation(b):
+        def variance(b):
             sum_p, sum_pp = sums[b]
             mean_sq = stat_pool.tile([P, STATS], F32, tag="mean_sq")
-            nc.scalar.activation(out=mean_sq[:], in_=sum_p[:], func=ACT.Square, scale=1.0 / K)
+            nc.vector.scalar_tensor_tensor(
+                out=mean_sq[:], in0=sum_p[:], scalar=1.0 / (K * K), in1=sum_p[:], op0=ALU.mult, op1=ALU.mult
+            )
             var = stat_pool.tile([P, STATS], F32, tag="var")
             nc.vector.scalar_tensor_tensor(
                 out=var[:], in0=sum_pp[:], scalar=1.0 / K, in1=mean_sq[:], op0=ALU.mult, op1=ALU.subtract
             )
+            variances[b] = var
+
+        def deviation(b):
             std = stat_pool.tile([P, STATS], F32, tag="std")
-            nc.scalar.activation(out=std[:], in_=var[:], func=ACT.Sqrt, bias=eps_col[:, 0:1])
+            nc.scalar.activation(out=std[:], in_=variances[b][:], func=ACT.Sqrt, bias=eps_col[:, 0:1])
             stds[b] = std
 
         def factors(b):
@@ -270,12 +273,7 @@ def tile_multiheadselfattention_pa_t_kernel(
             gain = gain_shift[:, j, qk * H + h : qk * H + h + 1]
             shift = gain_shift[:, j, SIDES + qk * H + h : SIDES + qk * H + h + 1]
             plane = planes_of[(b, side)][:, j, :]
-            if vector_empties(b, j):
-                nc.vector.tensor_scalar(
-                    out=plane, in0=flips[(b, side, j)][:], scalar1=gain, scalar2=shift, op0=ALU.mult, op1=ALU.add
-                )
-            else:
-                nc.scalar.activation(out=plane, in_=flips[(b, side, j)][:], func=ACT.Identity, scale=gain, bias=shift)
+            nc.scalar.activation(out=plane, in_=flips[(b, side, j)][:], func=ACT.Identity, scale=gain, bias=shift)
 
         def regroup(b, side):
             grouped = plane_pool.tile([P, T, PACK], BF16, tag="grouped", align_bytes=64)
@@ -326,9 +324,10 @@ def tile_multiheadselfattention_pa_t_kernel(
         TICKS = FRAME_TILES * PACK
         LAG_ACTIVATE = 4
         LAG_SQUARES = LAG_ACTIVATE + 1
-        LAG_DEVIATION = LAG_SQUARES + TICKS
-        LAG_FACTORS = LAG_DEVIATION + 1
-        LAG_NORMALISE = LAG_FACTORS + 2
+        LAG_VARIANCE = LAG_SQUARES + TICKS + 1
+        LAG_DEVIATION = LAG_VARIANCE + 1
+        LAG_FACTORS = LAG_DEVIATION + 2
+        LAG_NORMALISE = LAG_FACTORS + 1
         LAG_FLIP = LAG_NORMALISE + 5
         LAG_GAIN = LAG_FLIP + 1
         LAG_REGROUP = LAG_GAIN + 5
@@ -362,6 +361,9 @@ def tile_multiheadselfattention_pa_t_kernel(
             b, ft, side = piece(tick, LAG_SQUARES)
             if 0 <= b < B:
                 sum_squares(b, ft, side)
+            b, outer, inner = piece(tick, LAG_VARIANCE)
+            if 0 <= b < B and outer == 0 and inner == 0:
+                variance(b)
             b, outer, inner = piece(tick, LAG_DEVIATION)
             if 0 <= b < B and outer == 0 and inner == 0:
                 deviation(b)
@@ -369,8 +371,11 @@ def tile_multiheadselfattention_pa_t_kernel(
             if 0 <= b < B and outer == 0 and inner == 0:
                 factors(b)
             b, side, ft = piece(tick, LAG_NORMALISE)
-            if 0 <= b < B:
+            if 0 <= b < LAST:
                 normalise(b, side, ft)
+            elif b == LAST and side == 0:
+                for frame_tile in range(FRAME_TILES):
+                    normalise(b, ft, frame_tile)
             b, side, inner = piece(tick, LAG_REGROUP)
             if 0 <= b < B and inner == 0:
                 regroup(b, side)

@@ -26,6 +26,7 @@ LAST = B - 1
 RUN = 4
 AQ_AT, AK_AT, BQ_AT, BK_AT = 0, 16, 32, 32 + H * D
 ROW_WIDTH = BK_AT + H * D
+HELPED = 3
 SCALAR_BANKS = 7
 
 FLOPS = 2 * (2 * H * D) * C * (B * T * F) + 2 * B * H * T * T * K
@@ -48,15 +49,15 @@ def tile_multiheadselfattention_pa_t_kernel(
         flip_psum = ctx.enter_context(tc.psum_pool(name="flip_psum", bufs=3))
         score_psum = ctx.enter_context(tc.psum_pool(name="score_psum", bufs=2))
 
+        row = const.tile([P, ROW_WIDTH], BF16)
+        nc.vector.memset(row[:], 0.0)
+        nc.scalar.dma_start(out=row[0:1, AQ_AT : AQ_AT + H], in_=aq.unsqueeze(0))
+        nc.scalar.dma_start(out=row[0:1, AK_AT : AK_AT + H], in_=ak.unsqueeze(0))
+        nc.sync.dma_start(out=row[0:1, BQ_AT : BQ_AT + H * D], in_=bq.rearrange("h d -> (h d)").unsqueeze(0))
+        nc.sync.dma_start(out=row[0:1, BK_AT : BK_AT + H * D], in_=bk.rearrange("h d -> (h d)").unsqueeze(0))
         w_raw = const.tile([P, 2, C], BF16)
         nc.scalar.dma_start(out=w_raw[:, 0, :], in_=Wq.rearrange("h d c -> (h d) c"))
         nc.scalar.dma_start(out=w_raw[:, 1, :], in_=Wk.rearrange("h d c -> (h d) c"))
-        row = const.tile([P, ROW_WIDTH], BF16)
-        nc.vector.memset(row[:], 0.0)
-        nc.sync.dma_start(out=row[0:1, AQ_AT : AQ_AT + H], in_=aq.unsqueeze(0))
-        nc.sync.dma_start(out=row[0:1, AK_AT : AK_AT + H], in_=ak.unsqueeze(0))
-        nc.sync.dma_start(out=row[0:1, BQ_AT : BQ_AT + H * D], in_=bq.rearrange("h d -> (h d)").unsqueeze(0))
-        nc.sync.dma_start(out=row[0:1, BK_AT : BK_AT + H * D], in_=bk.rearrange("h d -> (h d)").unsqueeze(0))
         gs_raw = const.tile([P, K], BF16)
         nc.vector.memset(gs_raw[:], 0.0)
         nc.scalar.dma_start(out=gs_raw[0:2, :], in_=lwq.rearrange("h d f -> h (d f)"))
@@ -72,83 +73,91 @@ def tile_multiheadselfattention_pa_t_kernel(
                 nc.sync.dma_start(out=x_b[:, frames, :], in_=x[b, :, frames, :])
             x_sb.append(x_b)
 
-        ident = const.tile([P, P], F32)
-        make_identity(nc, ident[:])
-        eps_col = const.tile([P, 1], F32)
-        nc.vector.memset(eps_col[:], EPS)
-        warm_col = const.tile([P, 1], F32)
-        nc.scalar.activation(out=warm_col[:], in_=eps_col[:], func=ACT.Sqrt)
-
         ones_row = const.tile([P, P], BF16)
         nc.vector.memset(ones_row[:], 0.0)
         nc.vector.memset(ones_row[0:1, :], 1.0)
-        spread = flip_psum.tile([P, T], F32, tag="flip")
-        nc.tensor.matmul(out=spread[:, 0:ROW_WIDTH], lhsT=ones_row[:], rhs=row[:], start=True, stop=True)
+        eps_col = const.tile([P, 1], F32)
+        nc.vector.memset(eps_col[:], EPS)
+        ident = const.tile([P, P], F32)
+        make_identity(nc, ident[:])
+        warm_col = const.tile([P, 1], F32)
+        nc.scalar.activation(out=warm_col[:], in_=eps_col[:], func=ACT.Sqrt)
 
         slope = const.tile([P, SIDES], F32)
-        slope_by_head = slope[:].rearrange("p (h qk) -> p h qk", qk=2)
-        nc.vector.tensor_copy(out=slope_by_head[:, :, 0], in_=spread[:, AQ_AT : AQ_AT + H])
-        nc.vector.tensor_copy(out=slope_by_head[:, :, 1], in_=spread[:, AK_AT : AK_AT + H])
         sign = const.tile([P, SIDES], F32)
-        nc.vector.tensor_scalar(out=sign[:], in0=slope[:], scalar1=1.0, scalar2=2.0, op0=ALU.is_le, op1=ALU.mult)
-        nc.vector.tensor_scalar_add(out=sign[:], in0=sign[:], scalar1=-1.0)
-
-        bias_t = const.tile([P, SIDES, D_HI, F_HI, PACK], F32)
-        for side in range(SIDES):
-            h, qk = divmod(side, 2)
-            at = BQ_AT + (qk * H + h) * D
-            nc.vector.tensor_scalar_mul(
-                out=bias_t[:, side],
-                in0=spread[:, at : at + D]
-                .rearrange("p (dh dl) -> p dh dl", dl=PACK)
-                .unsqueeze(2)
-                .to_broadcast([P, D_HI, F_HI, PACK]),
-                scalar1=sign[:, side : side + 1],
-            )
-
-        bias_flip = flip_psum.tile([P, T], F32, tag="flip")
-        bias_flat = bias_t[:].rearrange("p s dh fh dl -> p (s dh fh dl)")
-        for block in range(SIDES):
-            cols = slice(block * P, (block + 1) * P)
-            nc.tensor.transpose(out=bias_flip[:, cols], in_=bias_flat[:, cols], identity=ident[:])
         bias_col = const.tile([P, SIDES], F32)
-        nc.vector.tensor_copy(out=bias_col[:], in_=bias_flip[:].rearrange("p (s t) -> p s t", s=SIDES)[:, :, 0])
-
-        w_f32 = const.tile([P, 2, C], F32)
-        nc.vector.tensor_copy(out=w_f32[:], in_=w_raw[:])
-        w_flip = flip_psum.tile([P, T], F32, tag="flip")
-        for qk in range(2):
-            nc.tensor.transpose(out=w_flip[:, qk * P : (qk + 1) * P], in_=w_f32[:, qk, :], identity=ident[:])
         w_t = const.tile([P, SIDES * D], BF16)
-        for side in range(SIDES):
-            h, qk = divmod(side, 2)
-            nc.vector.tensor_scalar_mul(
-                out=w_t[:, side * D : (side + 1) * D],
-                in0=w_flip[:, (qk * H + h) * D : (qk * H + h + 1) * D],
-                scalar1=sign[:, side : side + 1],
+
+        def prepare_convolution():
+            bias_row = const.tile([P, SIDES, D_HI, F_HI, PACK], BF16)
+            nc.vector.tensor_copy(
+                out=bias_row[:].rearrange("p s dh fh dl -> p (s dh) fh dl"),
+                in_=row[:, BQ_AT:ROW_WIDTH]
+                .rearrange("p (g dl) -> p g dl", dl=PACK)
+                .unsqueeze(2)
+                .to_broadcast([P, SIDES * D_HI, F_HI, PACK]),
+            )
+            spread = flip_psum.tile([P, T], F32, tag="flip")
+            nc.tensor.matmul(out=spread[:, 0:BQ_AT], lhsT=ones_row[:], rhs=row[:, 0:BQ_AT], start=True, stop=True)
+            for block in range(SIDES):
+                nc.tensor.matmul(
+                    out=spread[:, BQ_AT + block : BQ_AT + block + 1],
+                    lhsT=bias_row[:, block].rearrange("p dh fh dl -> p (dh fh dl)"),
+                    rhs=ones_row[:, 0:1],
+                    start=True,
+                    stop=True,
+                )
+
+            w_f32 = const.tile([P, 2, C], F32)
+            nc.vector.tensor_copy(out=w_f32[:], in_=w_raw[:])
+            w_flip = flip_psum.tile([P, T], F32, tag="flip")
+            for qk in range(2):
+                nc.tensor.transpose(out=w_flip[:, qk * P : (qk + 1) * P], in_=w_f32[:, qk, :], identity=ident[:])
+
+            slope_by_head = slope[:].rearrange("p (h qk) -> p h qk", qk=2)
+            nc.vector.tensor_copy(out=slope_by_head[:, :, 0], in_=spread[:, AQ_AT : AQ_AT + H])
+            nc.vector.tensor_copy(out=slope_by_head[:, :, 1], in_=spread[:, AK_AT : AK_AT + H])
+            nc.vector.tensor_scalar(out=sign[:], in0=slope[:], scalar1=1.0, scalar2=2.0, op0=ALU.is_le, op1=ALU.mult)
+            nc.vector.tensor_scalar_add(out=sign[:], in0=sign[:], scalar1=-1.0)
+
+            nc.vector.tensor_tensor(
+                out=bias_col[:].rearrange("p (h qk) -> p qk h", qk=2),
+                in0=spread[:, BQ_AT : BQ_AT + SIDES].rearrange("p (qk h) -> p qk h", qk=2),
+                in1=sign[:].rearrange("p (h qk) -> p qk h", qk=2),
+                op=ALU.mult,
             )
 
-        gs_rows = const.tile([P, PACK, D_HI, F_HI, PACK], F32)
-        gs_view = gs_raw[:].rearrange("p (dh dl fh j) -> p j dh fh dl", dl=PACK, fh=F_HI, j=PACK)
-        gs_flip = flip_psum.tile([P, T], F32, tag="flip")
-        for j in range(PACK):
-            nc.vector.tensor_copy(out=gs_rows[:, j], in_=gs_view[:, j])
-            nc.tensor.transpose(
-                out=gs_flip[:, j * P : (j + 1) * P],
-                in_=gs_rows[:, j].rearrange("p dh fh dl -> p (dh fh dl)"),
-                identity=ident[:],
-            )
+            for side in range(SIDES):
+                h, qk = divmod(side, 2)
+                nc.vector.tensor_scalar_mul(
+                    out=w_t[:, side * D : (side + 1) * D],
+                    in0=w_flip[:, (qk * H + h) * D : (qk * H + h + 1) * D],
+                    scalar1=sign[:, side : side + 1],
+                )
+
         gain_shift = const.tile([P, PACK, 2 * SIDES], F32)
-        nc.vector.tensor_copy(
-            out=gain_shift[:], in_=gs_flip[:].rearrange("p (j r) -> p j r", j=PACK)[:, :, 0 : 2 * SIDES]
-        )
-        for side in range(SIDES):
-            h, qk = divmod(side, 2)
-            nc.vector.tensor_scalar_mul(
-                out=gain_shift[:, :, qk * H + h],
-                in0=gain_shift[:, :, qk * H + h],
-                scalar1=sign[:, side : side + 1],
+
+        def prepare_gain_shift():
+            gs_rows = const.tile([P, PACK, D_HI, F_HI, PACK], F32)
+            gs_view = gs_raw[:].rearrange("p (dh dl fh j) -> p j dh fh dl", dl=PACK, fh=F_HI, j=PACK)
+            gs_flip = flip_psum.tile([P, T], F32, tag="flip")
+            for j in range(PACK):
+                nc.vector.tensor_copy(out=gs_rows[:, j], in_=gs_view[:, j])
+                nc.tensor.transpose(
+                    out=gs_flip[:, j * P : (j + 1) * P],
+                    in_=gs_rows[:, j].rearrange("p dh fh dl -> p (dh fh dl)"),
+                    identity=ident[:],
+                )
+            nc.vector.tensor_copy(
+                out=gain_shift[:], in_=gs_flip[:].rearrange("p (j r) -> p j r", j=PACK)[:, :, 0 : 2 * SIDES]
             )
+            for side in range(SIDES):
+                h, qk = divmod(side, 2)
+                nc.vector.tensor_scalar_mul(
+                    out=gain_shift[:, :, qk * H + h],
+                    in0=gain_shift[:, :, qk * H + h],
+                    scalar1=sign[:, side : side + 1],
+                )
 
         acts = {}
         sums = {}
@@ -161,8 +170,8 @@ def tile_multiheadselfattention_pa_t_kernel(
         mx_ops = {}
         score_banks = {}
 
-        def vector_empties(b, bank_number):
-            return b >= LAST - 2 and bank_number % 2 == 1
+        def vector_empties(b, h, ft):
+            return b > LAST - HELPED and ft % 2 == 1 and (b, h) != (LAST, 0)
 
         def convolve(b, ft, j):
             if ft == 0 and j == 0:
@@ -275,31 +284,36 @@ def tile_multiheadselfattention_pa_t_kernel(
             plane = planes_of[(b, side)][:, j, :]
             nc.scalar.activation(out=plane, in_=flips[(b, side, j)][:], func=ACT.Identity, scale=gain, bias=shift)
 
-        def regroup(b, side):
-            grouped = plane_pool.tile([P, T, PACK], BF16, tag="grouped", align_bytes=64)
+        def regroup(b, side, first, count):
+            if first == 0:
+                grouped_of[(b, side)] = plane_pool.tile([P, T, PACK], BF16, name="grouped", tag="grouped", align_bytes=64)
+            frames = slice(first * P, (first + count) * P)
             nc.vector.tensor_copy(
-                out=grouped[:].rearrange("p (c i) j -> p c j i", i=RUN),
-                in_=planes_of[(b, side)][:].rearrange("p j (c i) -> p c j i", i=RUN),
+                out=grouped_of[(b, side)][:, frames, :].rearrange("p (c i) j -> p c j i", i=RUN),
+                in_=planes_of[(b, side)][:, :, frames].rearrange("p j (c i) -> p c j i", i=RUN),
             )
-            grouped_of[(b, side)] = grouped
 
-        def quantise(b, side):
-            if side == 0:
+        def quantise(b, side, first, count):
+            if b not in mx_ops:
                 mx_ops[b] = (
                     code_pool.tile([P, SIDES, T], U32, name="words", tag="words", align_bytes=64),
                     code_pool.tile([P, SIDES, T], U8, name="scales", tag="scales", align_bytes=64),
                 )
             words, scales = mx_ops[b]
+            frames = slice(first * P, (first + count) * P)
             nc.vector.quantize_mx(
-                out=words[:, side, :].bitcast(FP8X4),
-                scales=scales[:, side, :],
-                in_=grouped_of[(b, side)][:].rearrange("p t j -> p (t j)"),
+                out=words[:, side, frames].bitcast(FP8X4),
+                scales=scales[:, side, frames],
+                in_=grouped_of[(b, side)][:, frames, :].rearrange("p t j -> p (t j)"),
             )
 
         def score(b, h, ft):
             words, scales = mx_ops[b]
             frames = slice(ft * P, (ft + 1) * P)
-            bank = score_psum.tile([P, T], F32, tag="score")
+            if b == LAST:
+                bank = conv_psum.tile([P, T], F32, name="late_score", tag="conv")
+            else:
+                bank = score_psum.tile([P, T], F32, name="score", tag="score")
             nc.tensor.matmul_mx(
                 out=bank[:],
                 lhsT=words[:, 2 * h, frames].bitcast(FP8X4),
@@ -313,7 +327,7 @@ def tile_multiheadselfattention_pa_t_kernel(
 
         def scale_and_store(b, h, ft):
             result = store_pool.tile([P, T], F32, tag="result")
-            if vector_empties(b, ft):
+            if vector_empties(b, h, ft):
                 nc.vector.tensor_scalar_mul(out=result[:], in0=score_banks[(b, h, ft)][:], scalar1=1.0 / math.sqrt(K))
             else:
                 nc.scalar.activation(
@@ -322,6 +336,7 @@ def tile_multiheadselfattention_pa_t_kernel(
             nc.sync.dma_start(out=out[b, h, ft * P : (ft + 1) * P, :], in_=result[:])
 
         TICKS = FRAME_TILES * PACK
+        SIDE_AT = (1, 0, 3, 2)
         LAG_ACTIVATE = 4
         LAG_SQUARES = LAG_ACTIVATE + 1
         LAG_VARIANCE = LAG_SQUARES + TICKS + 1
@@ -334,24 +349,25 @@ def tile_multiheadselfattention_pa_t_kernel(
         LAG_QUANTISE = LAG_REGROUP + 2
         LAG_SCORE = LAG_QUANTISE + 6
         LAG_STORE = LAG_SCORE + 1
+        TICK_GAIN_SHIFT = 8
 
         def piece(tick, lag):
             b, rest = divmod(tick - lag, TICKS)
             return (b,) + divmod(rest, 4)
 
-        for tick in range(B * TICKS + LAG_STORE):
+        def work_of(tick):
             b, ft, j = piece(tick, 0)
             if 0 <= b < B:
                 convolve(b, ft, j)
-            b, side, j = piece(tick, LAG_FLIP)
+            b, turn, j = piece(tick, LAG_FLIP)
             if 0 <= b < B:
-                flip(b, side, j)
+                flip(b, SIDE_AT[turn], j)
             b, outer, inner = piece(tick, LAG_SCORE)
             if 0 <= b < B and inner % 2 == 0:
                 score(b, *divmod(2 * outer + inner // 2, FRAME_TILES))
-            b, side, j = piece(tick, LAG_GAIN)
+            b, turn, j = piece(tick, LAG_GAIN)
             if 0 <= b < B:
-                gain_and_shift(b, side, j)
+                gain_and_shift(b, SIDE_AT[turn], j)
             b, outer, inner = piece(tick, LAG_STORE)
             if 0 <= b < B and inner % 2 == 0:
                 scale_and_store(b, *divmod(2 * outer + inner // 2, FRAME_TILES))
@@ -370,15 +386,29 @@ def tile_multiheadselfattention_pa_t_kernel(
             b, outer, inner = piece(tick, LAG_FACTORS)
             if 0 <= b < B and outer == 0 and inner == 0:
                 factors(b)
-            b, side, ft = piece(tick, LAG_NORMALISE)
+            b, turn, ft = piece(tick, LAG_NORMALISE)
             if 0 <= b < LAST:
-                normalise(b, side, ft)
-            elif b == LAST and side == 0:
+                normalise(b, SIDE_AT[turn], ft)
+            elif b == LAST and turn == 0:
                 for frame_tile in range(FRAME_TILES):
-                    normalise(b, ft, frame_tile)
-            b, side, inner = piece(tick, LAG_REGROUP)
+                    normalise(b, SIDE_AT[ft], frame_tile)
+            b, turn, inner = piece(tick, LAG_REGROUP)
             if 0 <= b < B and inner == 0:
-                regroup(b, side)
-            b, side, inner = piece(tick, LAG_QUANTISE)
-            if 0 <= b < B and inner == 0:
-                quantise(b, side)
+                if (b, turn) != (LAST, SIDES - 1):
+                    regroup(b, SIDE_AT[turn], 0, FRAME_TILES)
+                else:
+                    regroup(b, SIDE_AT[turn], 0, 2)
+                    regroup(b, SIDE_AT[turn], 2, 2)
+                    quantise(b, SIDE_AT[turn], 0, 2)
+                    quantise(b, SIDE_AT[turn], 2, 2)
+            b, turn, inner = piece(tick, LAG_QUANTISE)
+            if 0 <= b < B and inner == 0 and (b, turn) != (LAST, SIDES - 1):
+                quantise(b, SIDE_AT[turn], 0, FRAME_TILES)
+
+        with tc.manual_schedule(engines={mybir.EngineType.DVE, mybir.EngineType.PE}):
+            prepare_convolution()
+            for tick in range(TICK_GAIN_SHIFT):
+                work_of(tick)
+            prepare_gain_shift()
+        for tick in range(TICK_GAIN_SHIFT, B * TICKS + LAG_STORE):
+            work_of(tick)

@@ -27,7 +27,7 @@ RUN = 4
 AQ_AT, AK_AT, BQ_AT, BK_AT = 0, 16, 32, 32 + H * D
 ROW_WIDTH = BK_AT + H * D
 HELPED = 3
-SCALAR_BANKS = 7
+SCALAR_BANKS = (9, 10, 9, 7, 7, 7, 7, 7)
 
 FLOPS = 2 * (2 * H * D) * C * (B * T * F) + 2 * B * H * T * T * K
 
@@ -195,7 +195,7 @@ def tile_multiheadselfattention_pa_t_kernel(
                     start=False,
                     stop=(fh == F_HI - 1),
                 )
-            if ((ft * PACK + j) * SCALAR_BANKS) % (FRAME_TILES * PACK) < SCALAR_BANKS:
+            if ((ft * PACK + j) * SCALAR_BANKS[b]) % (FRAME_TILES * PACK) < SCALAR_BANKS[b]:
                 nc.scalar.copy(out=acts[b][:, ft, :, j, :], in_=by_side)
             else:
                 nc.vector.tensor_copy(out=acts[b][:, ft, :, j, :], in_=by_side)

@@ -161,6 +161,7 @@ def tile_multiheadselfattention_pa_t_kernel(
 
         acts = {}
         sums = {}
+        mean_of = {}
         variances = {}
         stds = {}
         norms = {}
@@ -228,15 +229,20 @@ def tile_multiheadselfattention_pa_t_kernel(
                 accum_out=sums[b][1][:, col : col + 1],
             )
 
-        def variance(b):
-            sum_p, sum_pp = sums[b]
+        def means(b):
+            sum_p = sums[b][0]
+            mean = stat_pool.tile([P, STATS], F32, tag="mean")
+            nc.vector.tensor_scalar_mul(out=mean[:], in0=sum_p[:], scalar1=1.0 / K)
             mean_sq = stat_pool.tile([P, STATS], F32, tag="mean_sq")
             nc.vector.scalar_tensor_tensor(
                 out=mean_sq[:], in0=sum_p[:], scalar=1.0 / (K * K), in1=sum_p[:], op0=ALU.mult, op1=ALU.mult
             )
+            mean_of[b] = (mean, mean_sq)
+
+        def variance(b):
             var = stat_pool.tile([P, STATS], F32, tag="var")
             nc.vector.scalar_tensor_tensor(
-                out=var[:], in0=sum_pp[:], scalar=1.0 / K, in1=mean_sq[:], op0=ALU.mult, op1=ALU.subtract
+                out=var[:], in0=sums[b][1][:], scalar=1.0 / K, in1=mean_of[b][1][:], op0=ALU.mult, op1=ALU.subtract
             )
             variances[b] = var
 
@@ -248,23 +254,18 @@ def tile_multiheadselfattention_pa_t_kernel(
         def factors(b):
             factor = stat_pool.tile([P, STATS], F32, tag="factor")
             nc.vector.reciprocal(out=factor[:], in_=stds[b][:])
-            offset = stat_pool.tile([P, STATS], F32, tag="offset")
-            nc.vector.scalar_tensor_tensor(
-                out=offset[:], in0=sums[b][0][:], scalar=-1.0 / K, in1=factor[:], op0=ALU.mult, op1=ALU.mult
-            )
-            norms[b] = (factor, offset)
+            norms[b] = factor
 
         def normalise(b, side, ft):
-            factor, offset = norms[b]
             col = ft * SIDES + side
             vals = acts[b][:, ft, side].rearrange("p j r -> p (j r)")
             nc.vector.tensor_scalar(
                 out=vals,
                 in0=vals,
-                scalar1=factor[:, col : col + 1],
-                scalar2=offset[:, col : col + 1],
-                op0=ALU.mult,
-                op1=ALU.add,
+                scalar1=mean_of[b][0][:, col : col + 1],
+                scalar2=norms[b][:, col : col + 1],
+                op0=ALU.subtract,
+                op1=ALU.mult,
             )
 
         def flip(b, side, j):
@@ -339,6 +340,7 @@ def tile_multiheadselfattention_pa_t_kernel(
         SIDE_AT = (1, 0, 3, 2)
         LAG_ACTIVATE = 4
         LAG_SQUARES = LAG_ACTIVATE + 1
+        LAG_MEANS = LAG_ACTIVATE + TICKS + 1
         LAG_VARIANCE = LAG_SQUARES + TICKS + 1
         LAG_DEVIATION = LAG_VARIANCE + 1
         LAG_FACTORS = LAG_DEVIATION + 2
@@ -377,6 +379,9 @@ def tile_multiheadselfattention_pa_t_kernel(
             b, ft, side = piece(tick, LAG_SQUARES)
             if 0 <= b < B:
                 sum_squares(b, ft, side)
+            b, outer, inner = piece(tick, LAG_MEANS)
+            if 0 <= b < B and outer == 0 and inner == 0:
+                means(b)
             b, outer, inner = piece(tick, LAG_VARIANCE)
             if 0 <= b < B and outer == 0 and inner == 0:
                 variance(b)

@@ -87,6 +87,7 @@ def tile_multiheadselfattention_pa_t_kernel(
         sign = const.tile([P, SIDES], F32)
         bias_col = const.tile([P, SIDES], F32)
         w_t = const.tile([P, SIDES * D], BF16)
+        bias_rows = const.tile([P, SIDES, P], F32)
 
         def prepare_convolution():
             bias_row = const.tile([P, SIDES, D_HI, F_HI, PACK], BF16)
@@ -126,6 +127,13 @@ def tile_multiheadselfattention_pa_t_kernel(
                 in1=sign[:].rearrange("p (h qk) -> p qk h", qk=2),
                 op=ALU.mult,
             )
+
+            bias_bank = flip_psum.tile([P, SIDES, P], F32, tag="flip")
+            for side in range(SIDES):
+                nc.tensor.transpose(
+                    out=bias_bank[:, side, :], in_=bias_col[:, side : side + 1].to_broadcast([P, P]), identity=ident[:]
+                )
+            nc.scalar.copy(out=bias_rows[:], in_=bias_bank[:])
 
             for side in range(SIDES):
                 h, qk = divmod(side, 2)
@@ -179,27 +187,29 @@ def tile_multiheadselfattention_pa_t_kernel(
                 acts[b] = act_pool.tile([P, FRAME_TILES, SIDES, PACK, P], F32, name="act", tag="act")
             bank = conv_psum.tile([P, SIDES * D_HI, F_HI, PACK], F32, tag="conv")
             by_side = bank[:].rearrange("p (s dh) fh dl -> p s (dh fh dl)", s=SIDES)
-            for side in range(SIDES):
-                nc.tensor.matmul(
-                    out=by_side[:, side, :],
-                    lhsT=bias_col[:, side : side + 1].to_broadcast([P, P]),
-                    rhs=ident[:],
-                    is_transpose=True,
-                    start=(side == 0),
-                    stop=False,
-                )
+            on_scalar = ((ft * PACK + j) * SCALAR_BANKS[b]) % (FRAME_TILES * PACK) < SCALAR_BANKS[b]
+            if on_scalar:
+                for side in range(SIDES):
+                    nc.tensor.matmul(
+                        out=by_side[:, side, :],
+                        lhsT=bias_col[:, side : side + 1].to_broadcast([P, P]),
+                        rhs=ident[:],
+                        is_transpose=True,
+                        start=(side == 0),
+                        stop=False,
+                    )
             for fh in range(F_HI):
                 nc.tensor.matmul(
                     out=bank[:, :, fh, :],
                     lhsT=x_sb[b][:, ft * P : (ft + 1) * P, fh * PACK + j],
                     rhs=w_t[:].rearrange("c (g dl) -> c g dl", dl=PACK),
-                    start=False,
-                    stop=(fh == F_HI - 1),
+                    start=not on_scalar,
+                    stop=(not on_scalar or fh == F_HI - 1),
                 )
-            if ((ft * PACK + j) * SCALAR_BANKS[b]) % (FRAME_TILES * PACK) < SCALAR_BANKS[b]:
+            if on_scalar:
                 nc.scalar.copy(out=acts[b][:, ft, :, j, :], in_=by_side)
             else:
-                nc.vector.tensor_copy(out=acts[b][:, ft, :, j, :], in_=by_side)
+                nc.vector.tensor_tensor(out=acts[b][:, ft, :, j, :], in0=by_side, in1=bias_rows[:], op=ALU.add)
 
         def activate(b, ft, side):
             if ft == 0 and side == 0:

@@ -80,6 +80,8 @@ def tile_multiheadselfattention_pa_t_kernel(
         nc.vector.memset(eps_col[:], EPS)
         ident = const.tile([P, P], F32)
         make_identity(nc, ident[:])
+        ident_bf16 = const.tile([P, P], BF16)
+        nc.gpsimd.tensor_copy(out=ident_bf16[:], in_=ident[:])
         warm_col = const.tile([P, 1], F32)
         nc.scalar.activation(out=warm_col[:], in_=eps_col[:], func=ACT.Sqrt)
 
@@ -109,22 +111,27 @@ def tile_multiheadselfattention_pa_t_kernel(
                     stop=True,
                 )
 
-            w_f32 = const.tile([P, 2, C], F32)
-            nc.vector.tensor_copy(out=w_f32[:], in_=w_raw[:])
-            w_flip = flip_psum.tile([P, T], F32, tag="flip")
+            w_flip = flip_psum.tile([P, 2, P], BF16, tag="flip")
             for qk in range(2):
-                nc.tensor.transpose(out=w_flip[:, qk * P : (qk + 1) * P], in_=w_f32[:, qk, :], identity=ident[:])
+                nc.tensor.transpose(out=w_flip[:, qk, :], in_=w_raw[:, qk, :], identity=ident_bf16[:])
 
-            slope_by_head = slope[:].rearrange("p (h qk) -> p h qk", qk=2)
-            nc.vector.tensor_copy(out=slope_by_head[:, :, 0], in_=spread[:, AQ_AT : AQ_AT + H])
-            nc.vector.tensor_copy(out=slope_by_head[:, :, 1], in_=spread[:, AK_AT : AK_AT + H])
-            nc.vector.tensor_scalar(out=sign[:], in0=slope[:], scalar1=1.0, scalar2=2.0, op0=ALU.is_le, op1=ALU.mult)
+            slopes_by_side = spread[:, 0:BQ_AT].rearrange("p (qk h) -> p h qk", qk=2)[:, 0:H, :]
+            sign_by_head = sign[:].rearrange("p (h qk) -> p h qk", qk=2)
+            nc.vector.tensor_scalar(
+                out=sign_by_head, in0=slopes_by_side, scalar1=1.0, scalar2=2.0, op0=ALU.is_le, op1=ALU.mult
+            )
             nc.vector.tensor_scalar_add(out=sign[:], in0=sign[:], scalar1=-1.0)
 
             nc.vector.tensor_tensor(
                 out=bias_col[:].rearrange("p (h qk) -> p qk h", qk=2),
                 in0=spread[:, BQ_AT : BQ_AT + SIDES].rearrange("p (qk h) -> p qk h", qk=2),
                 in1=sign[:].rearrange("p (h qk) -> p qk h", qk=2),
+                op=ALU.mult,
+            )
+            nc.vector.tensor_tensor(
+                out=w_t[:].rearrange("c (h qk d) -> c qk h d", h=H, qk=2),
+                in0=w_flip[:].rearrange("c qk (h d) -> c qk h d", h=H),
+                in1=sign[:].rearrange("p (h qk) -> p qk h", qk=2).unsqueeze(3).to_broadcast([P, 2, H, D]),
                 op=ALU.mult,
             )
 
@@ -134,14 +141,7 @@ def tile_multiheadselfattention_pa_t_kernel(
                     out=bias_bank[:, side, :], in_=bias_col[:, side : side + 1].to_broadcast([P, P]), identity=ident[:]
                 )
             nc.scalar.copy(out=bias_rows[:], in_=bias_bank[:])
-
-            for side in range(SIDES):
-                h, qk = divmod(side, 2)
-                nc.vector.tensor_scalar_mul(
-                    out=w_t[:, side * D : (side + 1) * D],
-                    in0=w_flip[:, (qk * H + h) * D : (qk * H + h + 1) * D],
-                    scalar1=sign[:, side : side + 1],
-                )
+            nc.vector.tensor_copy(out=slope[:].rearrange("p (h qk) -> p h qk", qk=2), in_=slopes_by_side)
 
         gain_shift = const.tile([P, PACK, 2 * SIDES], F32)
 

@@ -26,8 +26,10 @@ LAST = B - 1
 RUN = 4
 AQ_AT, AK_AT, BQ_AT, BK_AT = 0, 16, 32, 32 + H * D
 ROW_WIDTH = BK_AT + H * D
-HELPED = 3
-SCALAR_BANKS = (9, 10, 9, 7, 7, 7, 7, 7)
+HELPED = 2
+MOMENT_SIDES = (2, 3)
+MOMENT_BATCHES = range(1, B)
+SCALAR_BANKS = (9, 14, 16, 15, 15, 15, 15, 15)
 
 FLOPS = 2 * (2 * H * D) * C * (B * T * F) + 2 * B * H * T * T * K
 
@@ -169,6 +171,8 @@ def tile_multiheadselfattention_pa_t_kernel(
 
         acts = {}
         sums = {}
+        halves_of = {}
+        moments_of = {}
         mean_of = {}
         variances = {}
         stds = {}
@@ -211,13 +215,14 @@ def tile_multiheadselfattention_pa_t_kernel(
             else:
                 nc.vector.tensor_tensor(out=acts[b][:, ft, :, j, :], in0=by_side, in1=bias_rows[:], op=ALU.add)
 
+        def by_moments(b, side):
+            return b in MOMENT_BATCHES and side in MOMENT_SIDES
+
         def activate(b, ft, side):
             if ft == 0 and side == 0:
-                sums[b] = (
-                    stat_pool.tile([P, STATS], F32, name="sum_p", tag="sum_p"),
-                    stat_pool.tile([P, STATS], F32, name="sum_pp", tag="sum_pp"),
-                )
-            col = ft * SIDES + side
+                sums[b] = stat_pool.tile([P, 2, SIDES, FRAME_TILES], F32, name="sums", tag="sums")
+                halves_of[b] = stat_pool.tile([P, len(MOMENT_SIDES), FRAME_TILES, 2, 3], F32, name="halves", tag="halves")
+                moments_of[b] = stat_pool.tile([P, 2, len(MOMENT_SIDES) * FRAME_TILES, 2], F32, name="moments", tag="moments")
             vals = acts[b][:, ft, side].rearrange("p j r -> p (j r)")
             nc.vector.scalar_tensor_tensor(
                 out=vals,
@@ -226,33 +231,61 @@ def tile_multiheadselfattention_pa_t_kernel(
                 in1=vals,
                 op0=ALU.mult,
                 op1=ALU.max,
-                accum_out=sums[b][0][:, col : col + 1],
+                accum_out=None if by_moments(b, side) else sums[b][:, 0, side, ft : ft + 1],
             )
 
         def sum_squares(b, ft, side):
-            col = ft * SIDES + side
-            squares = junk_pool.tile([P, K], BF16, tag="squares")
-            nc.scalar.activation(
-                out=squares[:],
-                in_=acts[b][:, ft, side].rearrange("p j r -> p (j r)"),
-                func=ACT.Square,
-                accum_out=sums[b][1][:, col : col + 1],
+            vals = acts[b][:, ft, side].rearrange("p j r -> p (j r)")
+            if by_moments(b, side):
+                nc.vector.bn_stats(
+                    out=halves_of[b][:, MOMENT_SIDES.index(side), ft].rearrange("p half n -> p (half n)"), in_=vals
+                )
+            else:
+                squares = junk_pool.tile([P, K], BF16, tag="squares")
+                nc.scalar.activation(
+                    out=squares[:], in_=vals, func=ACT.Square, accum_out=sums[b][:, 1, side, ft : ft + 1]
+                )
+
+        def half_means(b):
+            return halves_of[b][:].rearrange("p s ft half n -> p (s ft) half n")[:, :, :, 1]
+
+        def half_sums(b):
+            nc.vector.tensor_scalar_mul(out=moments_of[b][:, 0], in0=half_means(b), scalar1=float(K // 2))
+
+        def half_squares(b):
+            nc.vector.tensor_tensor(out=moments_of[b][:, 1], in0=moments_of[b][:, 0], in1=half_means(b), op=ALU.mult)
+
+        def half_squares_about_zero(b):
+            nc.vector.tensor_tensor(
+                out=moments_of[b][:, 1],
+                in0=moments_of[b][:, 1],
+                in1=halves_of[b][:].rearrange("p s ft half n -> p (s ft) half n")[:, :, :, 2],
+                op=ALU.add,
+            )
+
+        def join_halves(b):
+            first = MOMENT_SIDES[0]
+            nc.vector.tensor_reduce(
+                out=sums[b][:, :, first : first + len(MOMENT_SIDES), :].rearrange("p kind s ft -> p kind (s ft)"),
+                in_=moments_of[b][:],
+                axis=mybir.AxisListType.X,
+                op=ALU.add,
             )
 
         def means(b):
-            sum_p = sums[b][0]
+            sum_p = sums[b][:, 0].rearrange("p s ft -> p (s ft)")
             mean = stat_pool.tile([P, STATS], F32, tag="mean")
-            nc.vector.tensor_scalar_mul(out=mean[:], in0=sum_p[:], scalar1=1.0 / K)
+            nc.vector.tensor_scalar_mul(out=mean[:], in0=sum_p, scalar1=1.0 / K)
             mean_sq = stat_pool.tile([P, STATS], F32, tag="mean_sq")
             nc.vector.scalar_tensor_tensor(
-                out=mean_sq[:], in0=sum_p[:], scalar=1.0 / (K * K), in1=sum_p[:], op0=ALU.mult, op1=ALU.mult
+                out=mean_sq[:], in0=sum_p, scalar=1.0 / (K * K), in1=sum_p, op0=ALU.mult, op1=ALU.mult
             )
             mean_of[b] = (mean, mean_sq)
 
         def variance(b):
             var = stat_pool.tile([P, STATS], F32, tag="var")
             nc.vector.scalar_tensor_tensor(
-                out=var[:], in0=sums[b][1][:], scalar=1.0 / K, in1=mean_of[b][1][:], op0=ALU.mult, op1=ALU.subtract
+                out=var[:], in0=sums[b][:, 1].rearrange("p s ft -> p (s ft)"), scalar=1.0 / K, in1=mean_of[b][1][:], op0=ALU.mult, op1=ALU.subtract
             )
             variances[b] = var
 
@@ -267,7 +300,7 @@ def tile_multiheadselfattention_pa_t_kernel(
             norms[b] = factor
 
         def normalise(b, side, ft):
-            col = ft * SIDES + side
+            col = side * FRAME_TILES + ft
             vals = acts[b][:, ft, side].rearrange("p j r -> p (j r)")
             nc.vector.tensor_scalar(
                 out=vals,
@@ -350,9 +383,10 @@ def tile_multiheadselfattention_pa_t_kernel(
         SIDE_AT = (1, 0, 3, 2)
         LAG_ACTIVATE = 4
         LAG_SQUARES = LAG_ACTIVATE + 1
-        LAG_MEANS = LAG_ACTIVATE + TICKS + 1
-        LAG_VARIANCE = LAG_SQUARES + TICKS + 1
-        LAG_DEVIATION = LAG_VARIANCE + 1
+        LAG_MOMENTS = LAG_SQUARES + TICKS
+        LAG_MEANS = LAG_MOMENTS + 1
+        LAG_VARIANCE = LAG_MEANS + 1
+        LAG_DEVIATION = LAG_VARIANCE
         LAG_FACTORS = LAG_DEVIATION + 2
         LAG_NORMALISE = LAG_FACTORS + 1
         LAG_FLIP = LAG_NORMALISE + 5
@@ -368,6 +402,14 @@ def tile_multiheadselfattention_pa_t_kernel(
             return (b,) + divmod(rest, 4)
 
         def work_of(tick):
+            b, outer, inner = piece(tick, LAG_MOMENTS)
+            if b in MOMENT_BATCHES and outer == 0 and inner == 0:
+                half_sums(b)
+            elif b in MOMENT_BATCHES and outer == 0 and inner == 1:
+                half_squares_about_zero(b)
+            b, outer, inner = piece(tick, LAG_VARIANCE)
+            if 0 <= b < B and outer == 0 and inner == 0:
+                variance(b)
             b, ft, j = piece(tick, 0)
             if 0 <= b < B:
                 convolve(b, ft, j)
@@ -389,12 +431,11 @@ def tile_multiheadselfattention_pa_t_kernel(
             b, ft, side = piece(tick, LAG_SQUARES)
             if 0 <= b < B:
                 sum_squares(b, ft, side)
-            b, outer, inner = piece(tick, LAG_MEANS)
-            if 0 <= b < B and outer == 0 and inner == 0:
-                means(b)
-            b, outer, inner = piece(tick, LAG_VARIANCE)
-            if 0 <= b < B and outer == 0 and inner == 0:
-                variance(b)
+            b, outer, inner = piece(tick, LAG_MOMENTS)
+            if b in MOMENT_BATCHES and outer == 0 and inner == 0:
+                half_squares(b)
+            elif b in MOMENT_BATCHES and outer == 0 and inner == 1:
+                join_halves(b)
             b, outer, inner = piece(tick, LAG_DEVIATION)
             if 0 <= b < B and outer == 0 and inner == 0:
                 deviation(b)
@@ -407,6 +448,9 @@ def tile_multiheadselfattention_pa_t_kernel(
             elif b == LAST and turn == 0:
                 for frame_tile in range(FRAME_TILES):
                     normalise(b, SIDE_AT[ft], frame_tile)
+            b, outer, inner = piece(tick, LAG_MEANS)
+            if 0 <= b < B and outer == 0 and inner == 0:
+                means(b)
             b, turn, inner = piece(tick, LAG_REGROUP)
             if 0 <= b < B and inner == 0:
                 if (b, turn) != (LAST, SIDES - 1):

import math
from contextlib import ExitStack

import concourse.mybir as mybir
from concourse.masks import make_identity

F32 = mybir.dt.float32
BF16 = mybir.dt.bfloat16
U32 = mybir.dt.uint32
U8 = mybir.dt.uint8
FP8X4 = mybir.dt.float8_e4m3fn_x4
ALU = mybir.AluOpType
ACT = mybir.ActivationFunctionType

B, C, T, F, H, D = 8, 128, 512, 8, 2, 64
P = 128
K = D * F
PACK = 4
EPS = 1e-5
FRAME_TILES = T // P
SIDES = 2 * H
F_HI = F // PACK
D_HI = D // PACK
STATS = FRAME_TILES * SIDES
LAST = B - 1
RUN = 4
AQ_AT, AK_AT, BQ_AT, BK_AT = 0, 16, 32, 32 + H * D
ROW_WIDTH = BK_AT + H * D
HELPED = 2
MOMENT_SIDES = (2, 3)
MOMENT_BATCHES = range(1, B)
SCALAR_BANKS = (9, 14, 16, 15, 15, 15, 15, 15)

FLOPS = 2 * (2 * H * D) * C * (B * T * F) + 2 * B * H * T * T * K


def tile_multiheadselfattention_pa_t_kernel(
    tc, x, Wq, bq, aq, lwq, lbq, Wk, bk, ak, lwk, lbk, out
):
    nc = tc.nc
    with ExitStack() as ctx:
        const = ctx.enter_context(tc.tile_pool(name="const", bufs=1))
        x_pool = ctx.enter_context(tc.tile_pool(name="x", bufs=1))
        act_pool = ctx.enter_context(tc.tile_pool(name="act", bufs=3))
        junk_pool = ctx.enter_context(tc.tile_pool(name="junk", bufs=4))
        stat_pool = ctx.enter_context(tc.tile_pool(name="stat", bufs=2))
        plane_pool = ctx.enter_context(tc.tile_pool(name="plane", bufs=2))
        code_pool = ctx.enter_context(tc.tile_pool(name="code", bufs=2))
        store_pool = ctx.enter_context(tc.tile_pool(name="store", bufs=8))
        conv_psum = ctx.enter_context(tc.psum_pool(name="conv_psum", bufs=3))
        flip_psum = ctx.enter_context(tc.psum_pool(name="flip_psum", bufs=3))
        score_psum = ctx.enter_context(tc.psum_pool(name="score_psum", bufs=2))

        row = const.tile([P, ROW_WIDTH], BF16)
        nc.vector.memset(row[:], 0.0)
        nc.scalar.dma_start(out=row[0:1, AQ_AT : AQ_AT + H], in_=aq.unsqueeze(0))
        nc.scalar.dma_start(out=row[0:1, AK_AT : AK_AT + H], in_=ak.unsqueeze(0))
        nc.sync.dma_start(out=row[0:1, BQ_AT : BQ_AT + H * D], in_=bq.rearrange("h d -> (h d)").unsqueeze(0))
        nc.sync.dma_start(out=row[0:1, BK_AT : BK_AT + H * D], in_=bk.rearrange("h d -> (h d)").unsqueeze(0))
        w_raw = const.tile([P, 2, C], BF16)
        nc.scalar.dma_start(out=w_raw[:, 0, :], in_=Wq.rearrange("h d c -> (h d) c"))
        nc.scalar.dma_start(out=w_raw[:, 1, :], in_=Wk.rearrange("h d c -> (h d) c"))
        gs_raw = const.tile([P, K], BF16)
        nc.vector.memset(gs_raw[:], 0.0)
        nc.scalar.dma_start(out=gs_raw[0:2, :], in_=lwq.rearrange("h d f -> h (d f)"))
        nc.scalar.dma_start(out=gs_raw[2:4, :], in_=lwk.rearrange("h d f -> h (d f)"))
        nc.scalar.dma_start(out=gs_raw[4:6, :], in_=lbq.rearrange("h d f -> h (d f)"))
        nc.scalar.dma_start(out=gs_raw[6:8, :], in_=lbk.rearrange("h d f -> h (d f)"))

        x_sb = []
        for b in range(B):
            x_b = x_pool.tile([P, T, F], BF16, name="x_b%d" % b)
            for ft in range(FRAME_TILES):
                frames = slice(ft * P, (ft + 1) * P)
                nc.sync.dma_start(out=x_b[:, frames, :], in_=x[b, :, frames, :])
            x_sb.append(x_b)

        ones_row = const.tile([P, P], BF16)
        nc.vector.memset(ones_row[:], 0.0)
        nc.vector.memset(ones_row[0:1, :], 1.0)
        eps_col = const.tile([P, 1], F32)
        nc.vector.memset(eps_col[:], EPS)
        ident = const.tile([P, P], F32)
        make_identity(nc, ident[:])
        ident_bf16 = const.tile([P, P], BF16)
        nc.gpsimd.tensor_copy(out=ident_bf16[:], in_=ident[:])
        warm_col = const.tile([P, 1], F32)
        nc.scalar.activation(out=warm_col[:], in_=eps_col[:], func=ACT.Sqrt)

        slope = const.tile([P, SIDES], F32)
        sign = const.tile([P, SIDES], F32)
        bias_col = const.tile([P, SIDES], F32)
        w_t = const.tile([P, SIDES * D], BF16)
        bias_rows = const.tile([P, SIDES, P], F32)

        def prepare_convolution():
            bias_row = const.tile([P, SIDES, D_HI, F_HI, PACK], BF16)
            nc.vector.tensor_copy(
                out=bias_row[:].rearrange("p s dh fh dl -> p (s dh) fh dl"),
                in_=row[:, BQ_AT:ROW_WIDTH]
                .rearrange("p (g dl) -> p g dl", dl=PACK)
                .unsqueeze(2)
                .to_broadcast([P, SIDES * D_HI, F_HI, PACK]),
            )
            spread = flip_psum.tile([P, T], F32, tag="flip")
            nc.tensor.matmul(out=spread[:, 0:BQ_AT], lhsT=ones_row[:], rhs=row[:, 0:BQ_AT], start=True, stop=True)
            for block in range(SIDES):
                nc.tensor.matmul(
                    out=spread[:, BQ_AT + block : BQ_AT + block + 1],
                    lhsT=bias_row[:, block].rearrange("p dh fh dl -> p (dh fh dl)"),
                    rhs=ones_row[:, 0:1],
                    start=True,
                    stop=True,
                )

            w_flip = flip_psum.tile([P, 2, P], BF16, tag="flip")
            for qk in range(2):
                nc.tensor.transpose(out=w_flip[:, qk, :], in_=w_raw[:, qk, :], identity=ident_bf16[:])

            slopes_by_side = spread[:, 0:BQ_AT].rearrange("p (qk h) -> p h qk", qk=2)[:, 0:H, :]
            sign_by_head = sign[:].rearrange("p (h qk) -> p h qk", qk=2)
            nc.vector.tensor_scalar(
                out=sign_by_head, in0=slopes_by_side, scalar1=1.0, scalar2=2.0, op0=ALU.is_le, op1=ALU.mult
            )
            nc.vector.tensor_scalar_add(out=sign[:], in0=sign[:], scalar1=-1.0)

            nc.vector.tensor_tensor(
                out=bias_col[:].rearrange("p (h qk) -> p qk h", qk=2),
                in0=spread[:, BQ_AT : BQ_AT + SIDES].rearrange("p (qk h) -> p qk h", qk=2),
                in1=sign[:].rearrange("p (h qk) -> p qk h", qk=2),
                op=ALU.mult,
            )
            nc.vector.tensor_tensor(
                out=w_t[:].rearrange("c (h qk d) -> c qk h d", h=H, qk=2),
                in0=w_flip[:].rearrange("c qk (h d) -> c qk h d", h=H),
                in1=sign[:].rearrange("p (h qk) -> p qk h", qk=2).unsqueeze(3).to_broadcast([P, 2, H, D]),
                op=ALU.mult,
            )

            bias_bank = flip_psum.tile([P, SIDES, P], F32, tag="flip")
            for side in range(SIDES):
                nc.tensor.transpose(
                    out=bias_bank[:, side, :], in_=bias_col[:, side : side + 1].to_broadcast([P, P]), identity=ident[:]
                )
            nc.scalar.copy(out=bias_rows[:], in_=bias_bank[:])
            nc.vector.tensor_copy(out=slope[:].rearrange("p (h qk) -> p h qk", qk=2), in_=slopes_by_side)

        gain_shift = const.tile([P, PACK, 2 * SIDES], F32)

        def prepare_gain_shift():
            gs_rows = const.tile([P, PACK, D_HI, F_HI, PACK], F32)
            gs_view = gs_raw[:].rearrange("p (dh dl fh j) -> p j dh fh dl", dl=PACK, fh=F_HI, j=PACK)
            gs_flip = flip_psum.tile([P, T], F32, tag="flip")
            for j in range(PACK):
                nc.vector.tensor_copy(out=gs_rows[:, j], in_=gs_view[:, j])
                nc.tensor.transpose(
                    out=gs_flip[:, j * P : (j + 1) * P],
                    in_=gs_rows[:, j].rearrange("p dh fh dl -> p (dh fh dl)"),
                    identity=ident[:],
                )
            nc.vector.tensor_copy(
                out=gain_shift[:], in_=gs_flip[:].rearrange("p (j r) -> p j r", j=PACK)[:, :, 0 : 2 * SIDES]
            )
            for side in range(SIDES):
                h, qk = divmod(side, 2)
                nc.vector.tensor_scalar_mul(
                    out=gain_shift[:, :, qk * H + h],
                    in0=gain_shift[:, :, qk * H + h],
                    scalar1=sign[:, side : side + 1],
                )

        acts = {}
        sums = {}
        halves_of = {}
        moments_of = {}
        mean_of = {}
        variances = {}
        stds = {}
        norms = {}
        flips = {}
        planes_of = {}
        grouped_of = {}
        mx_ops = {}
        score_banks = {}

        def vector_empties(b, h, ft):
            return b > LAST - HELPED and ft % 2 == 1 and (b, h) != (LAST, 0)

        def convolve(b, ft, j):
            if ft == 0 and j == 0:
                acts[b] = act_pool.tile([P, FRAME_TILES, SIDES, PACK, P], F32, name="act", tag="act")
            bank = conv_psum.tile([P, SIDES * D_HI, F_HI, PACK], F32, tag="conv")
            by_side = bank[:].rearrange("p (s dh) fh dl -> p s (dh fh dl)", s=SIDES)
            on_scalar = ((ft * PACK + j) * SCALAR_BANKS[b]) % (FRAME_TILES * PACK) < SCALAR_BANKS[b]
            if on_scalar:
                for side in range(SIDES):
                    nc.tensor.matmul(
                        out=by_side[:, side, :],
                        lhsT=bias_col[:, side : side + 1].to_broadcast([P, P]),
                        rhs=ident[:],
                        is_transpose=True,
                        start=(side == 0),
                        stop=False,
                    )
            for fh in range(F_HI):
                nc.tensor.matmul(
                    out=bank[:, :, fh, :],
                    lhsT=x_sb[b][:, ft * P : (ft + 1) * P, fh * PACK + j],
                    rhs=w_t[:].rearrange("c (g dl) -> c g dl", dl=PACK),
                    start=not on_scalar,
                    stop=(not on_scalar or fh == F_HI - 1),
                )
            if on_scalar:
                nc.scalar.copy(out=acts[b][:, ft, :, j, :], in_=by_side)
            else:
                nc.vector.tensor_tensor(out=acts[b][:, ft, :, j, :], in0=by_side, in1=bias_rows[:], op=ALU.add)

        def by_moments(b, side):
            return b in MOMENT_BATCHES and side in MOMENT_SIDES

        def activate(b, ft, side):
            if ft == 0 and side == 0:
                sums[b] = stat_pool.tile([P, 2, SIDES, FRAME_TILES], F32, name="sums", tag="sums")
                halves_of[b] = stat_pool.tile([P, len(MOMENT_SIDES), FRAME_TILES, 2, 3], F32, name="halves", tag="halves")
                moments_of[b] = stat_pool.tile([P, 2, len(MOMENT_SIDES) * FRAME_TILES, 2], F32, name="moments", tag="moments")
            vals = acts[b][:, ft, side].rearrange("p j r -> p (j r)")
            nc.vector.scalar_tensor_tensor(
                out=vals,
                in0=vals,
                scalar=slope[:, side : side + 1],
                in1=vals,
                op0=ALU.mult,
                op1=ALU.max,
                accum_out=None if by_moments(b, side) else sums[b][:, 0, side, ft : ft + 1],
            )

        def sum_squares(b, ft, side):
            vals = acts[b][:, ft, side].rearrange("p j r -> p (j r)")
            if by_moments(b, side):
                nc.vector.bn_stats(
                    out=halves_of[b][:, MOMENT_SIDES.index(side), ft].rearrange("p half n -> p (half n)"), in_=vals
                )
            else:
                squares = junk_pool.tile([P, K], BF16, tag="squares")
                nc.scalar.activation(
                    out=squares[:], in_=vals, func=ACT.Square, accum_out=sums[b][:, 1, side, ft : ft + 1]
                )

        def half_means(b):
            return halves_of[b][:].rearrange("p s ft half n -> p (s ft) half n")[:, :, :, 1]

        def half_sums(b):
            nc.vector.tensor_scalar_mul(out=moments_of[b][:, 0], in0=half_means(b), scalar1=float(K // 2))

        def half_squares(b):
            nc.vector.tensor_tensor(out=moments_of[b][:, 1], in0=moments_of[b][:, 0], in1=half_means(b), op=ALU.mult)

        def half_squares_about_zero(b):
            nc.vector.tensor_tensor(
                out=moments_of[b][:, 1],
                in0=moments_of[b][:, 1],
                in1=halves_of[b][:].rearrange("p s ft half n -> p (s ft) half n")[:, :, :, 2],
                op=ALU.add,
            )

        def join_halves(b):
            first = MOMENT_SIDES[0]
            nc.vector.tensor_reduce(
                out=sums[b][:, :, first : first + len(MOMENT_SIDES), :].rearrange("p kind s ft -> p kind (s ft)"),
                in_=moments_of[b][:],
                axis=mybir.AxisListType.X,
                op=ALU.add,
            )

        def means(b):
            sum_p = sums[b][:, 0].rearrange("p s ft -> p (s ft)")
            mean = stat_pool.tile([P, STATS], F32, tag="mean")
            nc.vector.tensor_scalar_mul(out=mean[:], in0=sum_p, scalar1=1.0 / K)
            mean_sq = stat_pool.tile([P, STATS], F32, tag="mean_sq")
            nc.vector.scalar_tensor_tensor(
                out=mean_sq[:], in0=sum_p, scalar=1.0 / (K * K), in1=sum_p, op0=ALU.mult, op1=ALU.mult
            )
            mean_of[b] = (mean, mean_sq)

        def variance(b):
            var = stat_pool.tile([P, STATS], F32, tag="var")
            nc.vector.scalar_tensor_tensor(
                out=var[:], in0=sums[b][:, 1].rearrange("p s ft -> p (s ft)"), scalar=1.0 / K, in1=mean_of[b][1][:], op0=ALU.mult, op1=ALU.subtract
            )
            variances[b] = var

        def deviation(b):
            std = stat_pool.tile([P, STATS], F32, tag="std")
            nc.scalar.activation(out=std[:], in_=variances[b][:], func=ACT.Sqrt, bias=eps_col[:, 0:1])
            stds[b] = std

        def factors(b):
            factor = stat_pool.tile([P, STATS], F32, tag="factor")
            nc.vector.reciprocal(out=factor[:], in_=stds[b][:])
            norms[b] = factor

        def normalise(b, side, ft):
            col = side * FRAME_TILES + ft
            vals = acts[b][:, ft, side].rearrange("p j r -> p (j r)")
            nc.vector.tensor_scalar(
                out=vals,
                in0=vals,
                scalar1=mean_of[b][0][:, col : col + 1],
                scalar2=norms[b][:, col : col + 1],
                op0=ALU.subtract,
                op1=ALU.mult,
            )

        def flip(b, side, j):
            flipped = flip_psum.tile([P, T], F32, tag="flip")
            for ft in range(FRAME_TILES):
                nc.tensor.transpose(
                    out=flipped[:, ft * P : (ft + 1) * P], in_=acts[b][:, ft, side, j, :], identity=ident[:]
                )
            flips[(b, side, j)] = flipped

        def gain_and_shift(b, side, j):
            if j == 0:
                planes_of[(b, side)] = plane_pool.tile([P, PACK, T], BF16, name="planes", tag="planes")
            h, qk = divmod(side, 2)
            gain = gain_shift[:, j, qk * H + h : qk * H + h + 1]
            shift = gain_shift[:, j, SIDES + qk * H + h : SIDES + qk * H + h + 1]
            plane = planes_of[(b, side)][:, j, :]
            nc.scalar.activation(out=plane, in_=flips[(b, side, j)][:], func=ACT.Identity, scale=gain, bias=shift)

        def regroup(b, side, first, count):
            if first == 0:
                grouped_of[(b, side)] = plane_pool.tile([P, T, PACK], BF16, name="grouped", tag="grouped", align_bytes=64)
            frames = slice(first * P, (first + count) * P)
            nc.vector.tensor_copy(
                out=grouped_of[(b, side)][:, frames, :].rearrange("p (c i) j -> p c j i", i=RUN),
                in_=planes_of[(b, side)][:, :, frames].rearrange("p j (c i) -> p c j i", i=RUN),
            )

        def quantise(b, side, first, count):
            if b not in mx_ops:
                mx_ops[b] = (
                    code_pool.tile([P, SIDES, T], U32, name="words", tag="words", align_bytes=64),
                    code_pool.tile([P, SIDES, T], U8, name="scales", tag="scales", align_bytes=64),
                )
            words, scales = mx_ops[b]
            frames = slice(first * P, (first + count) * P)
            nc.vector.quantize_mx(
                out=words[:, side, frames].bitcast(FP8X4),
                scales=scales[:, side, frames],
                in_=grouped_of[(b, side)][:, frames, :].rearrange("p t j -> p (t j)"),
            )

        def score(b, h, ft):
            words, scales = mx_ops[b]
            frames = slice(ft * P, (ft + 1) * P)
            if b == LAST:
                bank = conv_psum.tile([P, T], F32, name="late_score", tag="conv")
            else:
                bank = score_psum.tile([P, T], F32, name="score", tag="score")
            nc.tensor.matmul_mx(
                out=bank[:],
                lhsT=words[:, 2 * h, frames].bitcast(FP8X4),
                lhsT_scale=scales[:, 2 * h, frames],
                rhs=words[:, 2 * h + 1, :].bitcast(FP8X4),
                rhs_scale=scales[:, 2 * h + 1, :],
                start=True,
                stop=True,
            )
            score_banks[(b, h, ft)] = bank

        def scale_and_store(b, h, ft):
            result = store_pool.tile([P, T], F32, tag="result")
            if vector_empties(b, h, ft):
                nc.vector.tensor_scalar_mul(out=result[:], in0=score_banks[(b, h, ft)][:], scalar1=1.0 / math.sqrt(K))
            else:
                nc.scalar.activation(
                    out=result[:], in_=score_banks[(b, h, ft)][:], func=ACT.Copy, scale=1.0 / math.sqrt(K)
                )
            nc.sync.dma_start(out=out[b, h, ft * P : (ft + 1) * P, :], in_=result[:])

        TICKS = FRAME_TILES * PACK
        SIDE_AT = (1, 0, 3, 2)
        LAG_ACTIVATE = 4
        LAG_SQUARES = LAG_ACTIVATE + 1
        LAG_MOMENTS = LAG_SQUARES + TICKS
        LAG_MEANS = LAG_MOMENTS + 1
        LAG_VARIANCE = LAG_MEANS + 1
        LAG_DEVIATION = LAG_VARIANCE
        LAG_FACTORS = LAG_DEVIATION + 2
        LAG_NORMALISE = LAG_FACTORS + 1
        LAG_FLIP = LAG_NORMALISE + 5
        LAG_GAIN = LAG_FLIP + 1
        LAG_REGROUP = LAG_GAIN + 5
        LAG_QUANTISE = LAG_REGROUP + 2
        LAG_SCORE = LAG_QUANTISE + 6
        LAG_STORE = LAG_SCORE + 1
        TICK_GAIN_SHIFT = 8

        def piece(tick, lag):
            b, rest = divmod(tick - lag, TICKS)
            return (b,) + divmod(rest, 4)

        def work_of(tick):
            b, outer, inner = piece(tick, LAG_MOMENTS)
            if b in MOMENT_BATCHES and outer == 0 and inner == 0:
                half_sums(b)
            elif b in MOMENT_BATCHES and outer == 0 and inner == 1:
                half_squares_about_zero(b)
            b, outer, inner = piece(tick, LAG_VARIANCE)
            if 0 <= b < B and outer == 0 and inner == 0:
                variance(b)
            b, ft, j = piece(tick, 0)
            if 0 <= b < B:
                convolve(b, ft, j)
            b, turn, j = piece(tick, LAG_FLIP)
            if 0 <= b < B:
                flip(b, SIDE_AT[turn], j)
            b, outer, inner = piece(tick, LAG_SCORE)
            if 0 <= b < B and inner % 2 == 0:
                score(b, *divmod(2 * outer + inner // 2, FRAME_TILES))
            b, turn, j = piece(tick, LAG_GAIN)
            if 0 <= b < B:
                gain_and_shift(b, SIDE_AT[turn], j)
            b, outer, inner = piece(tick, LAG_STORE)
            if 0 <= b < B and inner % 2 == 0:
                scale_and_store(b, *divmod(2 * outer + inner // 2, FRAME_TILES))
            b, ft, side = piece(tick, LAG_ACTIVATE)
            if 0 <= b < B:
                activate(b, ft, side)
            b, ft, side = piece(tick, LAG_SQUARES)
            if 0 <= b < B:
                sum_squares(b, ft, side)
            b, outer, inner = piece(tick, LAG_MOMENTS)
            if b in MOMENT_BATCHES and outer == 0 and inner == 0:
                half_squares(b)
            elif b in MOMENT_BATCHES and outer == 0 and inner == 1:
                join_halves(b)
            b, outer, inner = piece(tick, LAG_DEVIATION)
            if 0 <= b < B and outer == 0 and inner == 0:
                deviation(b)
            b, outer, inner = piece(tick, LAG_FACTORS)
            if 0 <= b < B and outer == 0 and inner == 0:
                factors(b)
            b, turn, ft = piece(tick, LAG_NORMALISE)
            if 0 <= b < LAST:
                normalise(b, SIDE_AT[turn], ft)
            elif b == LAST and turn == 0:
                for frame_tile in range(FRAME_TILES):
                    normalise(b, SIDE_AT[ft], frame_tile)
            b, outer, inner = piece(tick, LAG_MEANS)
            if 0 <= b < B and outer == 0 and inner == 0:
                means(b)
            b, turn, inner = piece(tick, LAG_REGROUP)
            if 0 <= b < B and inner == 0:
                if (b, turn) != (LAST, SIDES - 1):
                    regroup(b, SIDE_AT[turn], 0, FRAME_TILES)
                else:
                    regroup(b, SIDE_AT[turn], 0, 2)
                    regroup(b, SIDE_AT[turn], 2, 2)
                    quantise(b, SIDE_AT[turn], 0, 2)
                    quantise(b, SIDE_AT[turn], 2, 2)
            b, turn, inner = piece(tick, LAG_QUANTISE)
            if 0 <= b < B and inner == 0 and (b, turn) != (LAST, SIDES - 1):
                quantise(b, SIDE_AT[turn], 0, FRAME_TILES)

        with tc.manual_schedule(engines={mybir.EngineType.DVE, mybir.EngineType.PE}):
            prepare_convolution()
            for tick in range(TICK_GAIN_SHIFT):
                work_of(tick)
            prepare_gain_shift()
        for tick in range(TICK_GAIN_SHIFT, B * TICKS + LAG_STORE):
            work_of(tick)
